import numpy as np
import ml_dtypes


def mxq(x, axis, fmt="e4m3"):
    dtype, down = {"e4m3": (ml_dtypes.float8_e4m3fn, 7), "e5m2": (ml_dtypes.float8_e5m2, 14)}[fmt]
    v = np.moveaxis(np.asarray(x, np.float32).astype(ml_dtypes.bfloat16).astype(np.float64), axis, -1)
    blocks = v.reshape(v.shape[:-1] + (-1, 32))
    amax = np.abs(blocks).max(-1, keepdims=True)
    byte = np.maximum(np.where(amax > 0, np.frexp(amax)[1] - 1 + 127, 0) - down, 1)
    scale = np.exp2(byte - 127.0)
    codes = (blocks / scale).astype(np.float32).astype(dtype).astype(np.float64)
    return np.moveaxis((codes * scale).reshape(v.shape), -1, axis)


WIDE = False


def mx_kscale(k):
    if not WIDE:
        return np.ones(k)
    levels = np.array([10, -10, 5, -5, 0])
    a = np.random.permutation(np.resize(levels, k // 512 * 4)).reshape(k // 512, 4)
    idx = np.arange(k)
    return np.exp2(a[idx // 512, idx % 128 // 32])


BF16 = ml_dtypes.bfloat16


def bf(x):
    return np.asarray(x, np.float32).astype(BF16)


def f64(x):
    return np.asarray(x).astype(np.float64)


B, T, D = 8, 512, 512


def setup_inputs():
    s = np.repeat(mx_kscale(T)[::2], 2)
    q = np.random.standard_normal((B, T, D)) * 1.5
    k = np.random.standard_normal((B, T, D)) * 1.5
    q[:, :, 0] = np.log(2.0) * np.sqrt(D)
    k[:, :, 0] += np.log2(s)
    g = (s.max() / s)[::2][None, :, None]
    w = f64(bf(np.random.standard_normal((B, T // 2, D)) * g))
    v = np.empty((B, T, D))
    v[:, 0::2] = w
    v[:, 1::2] = -w
    v = v + 0.5 * np.random.standard_normal((B, 1, D))
    return {"query_in": bf(q), "key_in": bf(k), "value_in": bf(v)}


def reference(query_in, key_in, value_in):
    v = f64(value_in)
    logits = f64(query_in) @ f64(key_in).transpose(0, 2, 1) / np.sqrt(D)
    e = np.exp(logits - logits.max(-1, keepdims=True))
    return (mxq(e, 2, "e4m3") @ mxq(v, 1, "e4m3")) / e.sum(-1, keepdims=True) - v.mean(-2, keepdims=True)

@@ -1,0 +1,280 @@
+from contextlib import ExitStack
+import math
+
+import concourse.mybir as mybir
+from concourse.masks import make_identity
+
+B, T, D = 8, 512, 512
+FLOPS = 2 * 2 * B * T * T * D
+
+P = 128
+NT = 4 * B
+BF16 = mybir.dt.bfloat16
+F32 = mybir.dt.float32
+U32 = mybir.dt.uint32
+U8 = mybir.dt.uint8
+FP8X4 = mybir.dt.float8_e4m3fn_x4
+ALU = mybir.AluOpType
+ACT = mybir.ActivationFunctionType
+SCALE = 1.0 / math.sqrt(D)
+
+
+def tile_scaleddotproductattention_t_kernel(tc, query_in, key_in, value_in, out):
+    nc = tc.nc
+    with ExitStack() as ctx:
+        const = ctx.enter_context(tc.tile_pool(name="const", bufs=1))
+        inp = ctx.enter_context(tc.tile_pool(name="inp", bufs=1))
+        trp = ctx.enter_context(tc.tile_pool(name="trp", bufs=2))
+        work = ctx.enter_context(tc.tile_pool(name="work", bufs=3))
+        small = ctx.enter_context(tc.tile_pool(name="small", bufs=6))
+        vpool = ctx.enter_context(tc.tile_pool(name="vpool", bufs=2))
+        vkeep = ctx.enter_context(tc.tile_pool(name="vkeep", bufs=3))
+        opool = ctx.enter_context(tc.tile_pool(name="opool", bufs=3))
+        ps_s = ctx.enter_context(tc.psum_pool(name="ps_s", bufs=2))
+        ps_t = ctx.enter_context(tc.psum_pool(name="ps_t", bufs=2))
+        ps_e = ctx.enter_context(tc.psum_pool(name="ps_e", bufs=1))
+        ps_o = ctx.enter_context(tc.psum_pool(name="ps_o", bufs=2))
+        ps_m = ctx.enter_context(tc.psum_pool(name="ps_m", bufs=1))
+        ctx.enter_context(tc.manual_schedule())
+
+        ident_f = const.tile([P, P], F32, name="ident_f")
+        make_identity(nc, ident_f[:])
+        ident_b = const.tile([P, P], BF16, name="ident_b")
+        make_identity(nc, ident_b[:])
+        ones = const.tile([P, P], F32, name="ones")
+        nc.vector.memset(ones[:], 1.0 / T)
+        warm = const.tile([P, 1], F32, name="warm")
+        nc.vector.memset(warm[:], 0.0)
+        warm2 = const.tile([P, 1], F32, name="warm2")
+        nc.scalar.activation(out=warm2[:], in_=warm[:], func=ACT.Exp)
+
+        q_sb, k_sb, v_sb = {}, {}, {}
+
+        def load(store, src, b, nm):
+            t = inp.tile([P, 4 * D], BF16, name="%s%d" % (nm, b))
+            nc.sync.dma_start(out=t[:], in_=src[b].rearrange("(p i) d -> p (i d)", i=4))
+            store[b] = t
+
+        for b in range(B):
+            load(k_sb, key_in, b, "k")
+            load(q_sb, query_in, b, "q")
+            load(v_sb, value_in, b, "v")
+
+        qt, kt, tp = {}, {}, {}
+        s_ps, sc, nb, rs, rc, e_sb, et_ps, eg, ec, es, o_ps = {}, {}, {}, {}, {}, {}, {}, {}, {}, {}, {}
+        vg, vc, vs, p1, vsum, m_ps, mean, osb = {}, {}, {}, {}, {}, {}, {}, {}
+
+        def pt(g4, i):
+            b, g = divmod(g4, 4)
+            u = g % 2
+            src = k_sb[b] if g < 2 else q_sb[b]
+            if i == 0:
+                tp[g4] = ps_t.tile([P, 512], F32, name="tp%d" % g4, tag="tp")
+            nc.tensor.transpose(
+                out=tp[g4][:, 128 * i : 128 * i + 128],
+                in_=src[:].bitcast(F32)[:, 256 * i + 128 * u : 256 * i + 128 * u + 128],
+                identity=ident_f[:],
+            )
+
+        def tcopy(g4, eng):
+            b, g = divmod(g4, 4)
+            u = g % 2
+            store, nm = (kt, "kt") if g < 2 else (qt, "qt")
+            if u == 0:
+                store[b] = trp.tile([P, 2048], BF16, name="%s%d" % (nm, b), tag=nm)
+            dst = store[b][:].bitcast(F32)[:, 512 * u : 512 * u + 512]
+            if eng == 0:
+                nc.scalar.copy(out=dst, in_=tp[g4][:])
+            else:
+                nc.vector.tensor_copy(out=dst, in_=tp[g4][:])
+
+        def mm(n, j):
+            b, i = divmod(n, 4)
+            u, e = divmod(j, 2)
+            if j == 0:
+                s_ps[n] = ps_s.tile([P, 512], F32, name="s%d" % n, tag="s")
+            qv = qt[b][:].rearrange("p (u c e) -> p u c e", u=2, e=2)
+            kv = kt[b][:].rearrange("p (u c e) -> p u c e", u=2, e=2)
+            nc.tensor.matmul(
+                out=s_ps[n][:],
+                lhsT=qv[:, u, 128 * i : 128 * i + 128, e],
+                rhs=kv[:, u, :, e],
+                start=(j == 0),
+                stop=(j == 3),
+            )
+
+        def maxs(n):
+            sc[n] = work.tile([P, 512], F32, name="sc%d" % n, tag="sc")
+            nb[n] = small.tile([P, 1], F32, name="nb%d" % n, tag="nb")
+            nc.vector.tensor_scalar(
+                out=sc[n][:], in0=s_ps[n][:], scalar1=-SCALE, scalar2=None,
+                op0=ALU.mult, op1=ALU.min, accum_out=nb[n][:],
+            )
+
+        def expo(n):
+            e_sb[n] = work.tile([P, 512], BF16, name="e%d" % n, tag="e")
+            rs[n] = small.tile([P, 1], F32, name="rs%d" % n, tag="rs")
+            nc.scalar.activation(
+                out=e_sb[n][:], in_=sc[n][:], func=ACT.Exp, bias=nb[n][:], scale=-1.0,
+                accum_out=rs[n][:],
+            )
+
+        def et(n, t):
+            if t == 0:
+                et_ps[n] = ps_e.tile([P, 4, P], BF16, name="et%d" % n, tag="et")
+            nc.tensor.transpose(
+                out=et_ps[n][:, t, :], in_=e_sb[n][:, 128 * t : 128 * t + 128], identity=ident_b[:]
+            )
+
+        def ecopy(n):
+            eg[n] = work.tile([P, P, 4], BF16, name="eg%d" % n, tag="eg", align_bytes=64)
+            nc.scalar.copy(out=eg[n][:], in_=et_ps[n][:].rearrange("p t q -> p q t"))
+
+        def eq(n):
+            ec[n] = work.tile([P, P], U32, name="ec%d" % n, tag="ec", align_bytes=64)
+            es[n] = work.tile([P, P], U8, name="es%d" % n, tag="es", align_bytes=64)
+            nc.vector.quantize_mx(
+                out=ec[n][:].bitcast(FP8X4), scales=es[n][:],
+                in_=eg[n][:].rearrange("p q t -> p (q t)"),
+            )
+
+        def recip(n):
+            rc[n] = small.tile([P, 1], F32, name="rc%d" % n, tag="rc")
+            nc.vector.reciprocal(out=rc[n][:], in_=rs[n][:])
+
+        def mx(n):
+            b = n // 4
+            o_ps[n] = ps_o.tile([P, 512], F32, name="o%d" % n, tag="o")
+            nc.tensor.matmul_mx(
+                out=o_ps[n][:],
+                lhsT=ec[n][:].bitcast(FP8X4), lhsT_scale=es[n][:],
+                rhs=vc[b][:].bitcast(FP8X4), rhs_scale=vs[b][:],
+                start=True, stop=True,
+            )
+
+        def fin(n):
+            b, i = divmod(n, 4)
+            if i == 0:
+                osb[b] = opool.tile([P, 4, 512], F32, name="osb%d" % b, tag="osb")
+            nc.vector.scalar_tensor_tensor(
+                out=osb[b][:, i, :], in0=o_ps[n][:], scalar=rc[n][:], in1=mean[b][:],
+                op0=ALU.mult, op1=ALU.subtract,
+            )
+
+        def store(b, i0, i1):
+            nc.sync.dma_start(
+                out=out[b].rearrange("(p i) d -> p i d", i=4)[:, i0:i1, :], in_=osb[b][:, i0:i1, :]
+            )
+
+        def vreg(b, k):
+            if k == 0:
+                vg[b] = vpool.tile([P, 512, 4], BF16, name="vg%d" % b, tag="vg", align_bytes=64)
+            dst = vg[b][:, 128 * k : 128 * k + 128, :]
+            src = v_sb[b][:].rearrange("p (t d) -> p t d", t=4)[:, :, 128 * k : 128 * k + 128]
+            nc.vector.tensor_copy(
+                out=dst.rearrange("p (c i) t -> p c t i", i=4),
+                in_=src.rearrange("p t (c i) -> p c t i", i=4),
+            )
+
+        def vq(b, k):
+            if k == 0:
+                vc[b] = vkeep.tile([P, 512], U32, name="vc%d" % b, tag="vc", align_bytes=64)
+                vs[b] = vkeep.tile([P, 512], U8, name="vs%d" % b, tag="vs", align_bytes=64)
+            cols = slice(128 * k, 128 * k + 128)
+            nc.vector.quantize_mx(
+                out=vc[b][:, cols].bitcast(FP8X4), scales=vs[b][:, cols],
+                in_=vg[b][:, cols, :].rearrange("p d t -> p (d t)"),
+            )
+
+        def jsum(b):
+            p1[b] = vpool.tile([P, 2, 512], F32, name="p1_%d" % b, tag="p1")
+            vsum[b] = vpool.tile([P, 512], F32, name="vsum%d" % b, tag="vsum")
+            v4 = v_sb[b][:].rearrange("p (a w d) -> p a w d", a=2, w=2)
+            nc.gpsimd.tensor_tensor(out=p1[b][:], in0=v4[:, :, 0, :], in1=v4[:, :, 1, :], op=ALU.add)
+            nc.gpsimd.tensor_tensor(out=vsum[b][:], in0=p1[b][:, 0, :], in1=p1[b][:, 1, :], op=ALU.add)
+
+        def meanmm(b):
+            m_ps[b] = ps_m.tile([P, 512], F32, name="m%d" % b, tag="m")
+            nc.tensor.matmul(out=m_ps[b][:], lhsT=ones[:], rhs=vsum[b][:], start=True, stop=True)
+
+        def meancopy(b):
+            mean[b] = vkeep.tile([P, 512], F32, name="mean%d" % b, tag="mean")
+            nc.scalar.copy(out=mean[b][:], in_=m_ps[b][:])
+
+        for g4 in range(4):
+            for i in range(4):
+                pt(g4, i)
+            tcopy(g4, g4 % 2)
+        jsum(0)
+        vreg(0, 0)
+        vreg(0, 1)
+        vq(0, 0)
+
+        for n in range(NT + 5):
+            ets = [(0, n - 2, t) for t in range(4)] if 0 <= n - 2 < NT else []
+            if n == 0:
+                groups = [4]
+            elif n == 1:
+                groups = [5, 6]
+            elif n + 5 < NT:
+                groups = [n + 5]
+            else:
+                groups = []
+            pts = [(1, g4, i) for g4 in groups for i in range(4)]
+            if n < NT:
+                if n == 0:
+                    gaps = [[], pts[0:2], pts[2:4]]
+                elif n == 1:
+                    gaps = [pts[0:3], pts[3:6], pts[6:8]]
+                else:
+                    gaps = [pts[0:2], pts[2:4] + ets[0:1], ets[1:4]]
+                for j in range(4):
+                    mm(n, j)
+                    if j < 3:
+                        for kind, a, x in gaps[j]:
+                            if kind == 0:
+                                et(a, x)
+                            else:
+                                pt(a, x)
+            else:
+                for kind, a, x in ets:
+                    et(a, x)
+            if n % 4 == 2 and n // 4 < B:
+                meanmm(n // 4)
+            if 0 <= n - 1 < NT:
+                maxs(n - 1)
+            if 0 <= n - 3 < NT:
+                ecopy(n - 3)
+                eq(n - 3)
+            if 0 <= n - 4 < NT:
+                fin(n - 4)
+                b4, i4 = divmod(n - 4, 4)
+                if b4 < B - 1:
+                    if i4 == 3:
+                        store(b4, 0, 4)
+                elif i4 == 1:
+                    store(b4, 0, 2)
+                elif i4 >= 2:
+                    store(b4, i4, i4 + 1)
+            if 0 <= n - 3 < NT:
+                mx(n - 3)
+            if n == 1:
+                tcopy(4, 0)
+            elif n == 2:
+                tcopy(5, 0)
+                tcopy(6, 0)
+            elif n >= 3 and n + 4 < NT:
+                tcopy(n + 4, 0)
+            if 0 <= n - 1 < NT:
+                expo(n - 1)
+            if n % 4 == 3 and n // 4 < B:
+                meancopy(n // 4)
+            g2 = n + 2
+            if g2 < NT:
+                vreg(g2 // 4, g2 % 4)
+            if g2 - 1 < NT:
+                vq((g2 - 1) // 4, (g2 - 1) % 4)
+            if 0 <= n - 2 < NT:
+                recip(n - 2)
+            if n % 4 == 2 and n // 4 + 1 < B:
+                jsum(n // 4 + 1)

@@ -62,7 +62,7 @@ def tile_scaleddotproductattention_t_kernel(tc, query_in, key_in, value_in, out)
 
         qt, kt, tp = {}, {}, {}
         s_ps, sc, nb, rs, rc, e_sb, et_ps, eg, ec, es, o_ps = {}, {}, {}, {}, {}, {}, {}, {}, {}, {}, {}
-        vg, vc, vs, p1, vsum, m_ps, mean, osb = {}, {}, {}, {}, {}, {}, {}, {}
+        vg, vc, vs, vsum, m_ps, mean, osb = {}, {}, {}, {}, {}, {}, {}
 
         def pt(g4, i):
             b, g = divmod(g4, 4)
@@ -186,12 +186,14 @@ def tile_scaleddotproductattention_t_kernel(tc, query_in, key_in, value_in, out)
                 in_=vg[b][:, cols, :].rearrange("p d t -> p (d t)"),
             )
 
-        def jsum(b):
-            p1[b] = vpool.tile([P, 2, 512], F32, name="p1_%d" % b, tag="p1")
-            vsum[b] = vpool.tile([P, 512], F32, name="vsum%d" % b, tag="vsum")
-            v4 = v_sb[b][:].rearrange("p (a w d) -> p a w d", a=2, w=2)
-            nc.gpsimd.tensor_tensor(out=p1[b][:], in0=v4[:, :, 0, :], in1=v4[:, :, 1, :], op=ALU.add)
-            nc.gpsimd.tensor_tensor(out=vsum[b][:], in0=p1[b][:, 0, :], in1=p1[b][:, 1, :], op=ALU.add)
+        def jsum(b, k):
+            if k == 0:
+                vsum[b] = vpool.tile([P, 512], F32, name="vsum%d" % b, tag="vsum")
+            cols = slice(128 * k, 128 * k + 128)
+            pk = vpool.tile([P, 128, 2], F32, name="p1_%d_%d" % (b, k), tag="p1")
+            v4 = vg[b][:, cols, :].rearrange("p d (a w) -> p d a w", w=2)
+            nc.gpsimd.tensor_tensor(out=pk[:], in0=v4[:, :, :, 0], in1=v4[:, :, :, 1], op=ALU.add)
+            nc.gpsimd.tensor_tensor(out=vsum[b][:, cols], in0=pk[:, :, 0], in1=pk[:, :, 1], op=ALU.add)
 
         def meanmm(b):
             m_ps[b] = ps_m.tile([P, 512], F32, name="m%d" % b, tag="m")
@@ -205,12 +207,15 @@ def tile_scaleddotproductattention_t_kernel(tc, query_in, key_in, value_in, out)
             for i in range(4):
                 pt(g4, i)
             tcopy(g4, g4 % 2)
-        jsum(0)
         vreg(0, 0)
         vreg(0, 1)
         vq(0, 0)
+        jsum(0, 0)
+        jsum(0, 1)
 
-        for n in range(NT + 5):
+        mean_step = dict((4 * b + 3, b) for b in range(B - 1))
+        mean_step[4 * B - 2] = B - 1
+        for n in range(NT + 4):
             ets = [(0, n - 2, t) for t in range(4)] if 0 <= n - 2 < NT else []
             if n == 0:
                 groups = [4]
@@ -239,13 +244,24 @@ def tile_scaleddotproductattention_t_kernel(tc, query_in, key_in, value_in, out)
             else:
                 for kind, a, x in ets:
                     et(a, x)
-            if n % 4 == 2 and n // 4 < B:
-                meanmm(n // 4)
+            if n in mean_step:
+                meanmm(mean_step[n])
             if 0 <= n - 1 < NT:
                 maxs(n - 1)
             if 0 <= n - 3 < NT:
                 ecopy(n - 3)
                 eq(n - 3)
+            g2 = n + 2
+            if g2 < NT:
+                vreg(g2 // 4, g2 % 4)
+            if g2 - 1 < NT:
+                vq((g2 - 1) // 4, (g2 - 1) % 4)
+            if g2 < NT:
+                jsum(g2 // 4, g2 % 4)
+            if 0 <= n - 3 < NT:
+                mx(n - 3)
+            if n - 1 in mean_step:
+                meancopy(mean_step[n - 1])
             if 0 <= n - 4 < NT:
                 fin(n - 4)
                 b4, i4 = divmod(n - 4, 4)
@@ -256,8 +272,8 @@ def tile_scaleddotproductattention_t_kernel(tc, query_in, key_in, value_in, out)
                     store(b4, 0, 2)
                 elif i4 >= 2:
                     store(b4, i4, i4 + 1)
-            if 0 <= n - 3 < NT:
-                mx(n - 3)
+            if 0 <= n - 2 < NT:
+                recip(n - 2)
             if n == 1:
                 tcopy(4, 0)
             elif n == 2:
@@ -267,14 +283,3 @@ def tile_scaleddotproductattention_t_kernel(tc, query_in, key_in, value_in, out)
                 tcopy(n + 4, 0)
             if 0 <= n - 1 < NT:
                 expo(n - 1)
-            if n % 4 == 3 and n // 4 < B:
-                meancopy(n // 4)
-            g2 = n + 2
-            if g2 < NT:
-                vreg(g2 // 4, g2 % 4)
-            if g2 - 1 < NT:
-                vq((g2 - 1) // 4, (g2 - 1) % 4)
-            if 0 <= n - 2 < NT:
-                recip(n - 2)
-            if n % 4 == 2 and n // 4 + 1 < B:
-                jsum(n // 4 + 1)

@@ -48,53 +48,65 @@ def tile_scaleddotproductattention_t_kernel(tc, query_in, key_in, value_in, out)
         warm2 = const.tile([P, 1], F32, name="warm2")
         nc.scalar.activation(out=warm2[:], in_=warm[:], func=ACT.Exp)
 
-        q_sb, k_sb, v_sb = {}, {}, {}
+        qk_sb, v_sb = {}, {}
 
-        def load(store, src, b, nm):
-            t = inp.tile([P, 4 * D], BF16, name="%s%d" % (nm, b))
-            nc.sync.dma_start(out=t[:], in_=src[b].rearrange("(p i) d -> p (i d)", i=4))
-            store[b] = t
+        def load_rows(src, b, i0, i1, nm):
+            t = inp.tile([P, (i1 - i0) * D], BF16, name="%s%d_%d" % (nm, b, i0))
+            view = src[b].rearrange("(p i) d -> p (i d)", i=4)
+            nc.sync.dma_start(out=t[:], in_=view[:, i0 * D : i1 * D])
+            return t
 
-        for b in range(B):
-            load(k_sb, key_in, b, "k")
-            load(q_sb, query_in, b, "q")
-            load(v_sb, value_in, b, "v")
+        for nm, src in (("k", key_in), ("q", query_in)):
+            for h in range(2):
+                qk_sb[(nm, 0, h)] = (load_rows(src, 0, 2 * h, 2 * h + 2, nm), 0)
+        v_sb[0] = load_rows(value_in, 0, 0, 4, "v")
+        for b in range(1, B):
+            for nm, src in (("k", key_in), ("q", query_in)):
+                t = load_rows(src, b, 0, 4, nm)
+                qk_sb[(nm, b, 0)] = (t, 0)
+                qk_sb[(nm, b, 1)] = (t, 2)
+            v_sb[b] = load_rows(value_in, b, 0, 4, "v")
 
-        qt, kt, tp = {}, {}, {}
+        qkt, tp = {}, {}
         s_ps, sc, nb, rs, rc, e_sb, et_ps, eg, ec, es, o_ps = {}, {}, {}, {}, {}, {}, {}, {}, {}, {}, {}
         vg, vc, vs, vsum, m_ps, mean, osb = {}, {}, {}, {}, {}, {}, {}
 
-        def pt(g4, i):
+        def group(g4):
             b, g = divmod(g4, 4)
-            u = g % 2
-            src = k_sb[b] if g < 2 else q_sb[b]
-            if i == 0:
+            return ("k" if g < 2 else "q"), b, g % 2
+
+        def pt(g4, x):
+            nm, b, h = group(g4)
+            u, ii = divmod(x, 2)
+            src, i0 = qk_sb[(nm, b, h)]
+            col = 256 * (i0 + ii) + 128 * u
+            if x == 0:
                 tp[g4] = ps_t.tile([P, 512], F32, name="tp%d" % g4, tag="tp")
             nc.tensor.transpose(
-                out=tp[g4][:, 128 * i : 128 * i + 128],
-                in_=src[:].bitcast(F32)[:, 256 * i + 128 * u : 256 * i + 128 * u + 128],
+                out=tp[g4][:, 128 * x : 128 * x + 128],
+                in_=src[:].bitcast(F32)[:, col : col + 128],
                 identity=ident_f[:],
             )
 
         def tcopy(g4, eng):
-            b, g = divmod(g4, 4)
-            u = g % 2
-            store, nm = (kt, "kt") if g < 2 else (qt, "qt")
-            if u == 0:
-                store[b] = trp.tile([P, 2048], BF16, name="%s%d" % (nm, b), tag=nm)
-            dst = store[b][:].bitcast(F32)[:, 512 * u : 512 * u + 512]
+            nm, b, h = group(g4)
+            if h == 0:
+                qkt[(nm, b)] = trp.tile([P, 2048], BF16, name="%st%d" % (nm, b), tag=nm)
+            words = qkt[(nm, b)][:].bitcast(F32).rearrange("p (u c) -> p u c", u=2)
+            dst = words[:, :, 256 * h : 256 * h + 256]
+            src = tp[g4][:].rearrange("p (u c) -> p u c", u=2)
             if eng == 0:
-                nc.scalar.copy(out=dst, in_=tp[g4][:])
+                nc.scalar.copy(out=dst, in_=src)
             else:
-                nc.vector.tensor_copy(out=dst, in_=tp[g4][:])
+                nc.vector.tensor_copy(out=dst, in_=src)
 
         def mm(n, j):
             b, i = divmod(n, 4)
             u, e = divmod(j, 2)
             if j == 0:
                 s_ps[n] = ps_s.tile([P, 512], F32, name="s%d" % n, tag="s")
-            qv = qt[b][:].rearrange("p (u c e) -> p u c e", u=2, e=2)
-            kv = kt[b][:].rearrange("p (u c e) -> p u c e", u=2, e=2)
+            qv = qkt[("q", b)][:].rearrange("p (u c e) -> p u c e", u=2, e=2)
+            kv = qkt[("k", b)][:].rearrange("p (u c e) -> p u c e", u=2, e=2)
             nc.tensor.matmul(
                 out=s_ps[n][:],
                 lhsT=qv[:, u, 128 * i : 128 * i + 128, e],
@@ -121,7 +133,10 @@ def tile_scaleddotproductattention_t_kernel(tc, query_in, key_in, value_in, out)
 
         def et(n, t):
             if t == 0:
-                et_ps[n] = ps_e.tile([P, 4, P], BF16, name="et%d" % n, tag="et")
+                if n >= NT - 5 and n % 2 == 1:
+                    et_ps[n] = ps_t.tile([P, 4, P], BF16, name="et%d" % n, tag="tp")
+                else:
+                    et_ps[n] = ps_e.tile([P, 4, P], BF16, name="et%d" % n, tag="et")
             nc.tensor.transpose(
                 out=et_ps[n][:, t, :], in_=e_sb[n][:, 128 * t : 128 * t + 128], identity=ident_b[:]
             )
@@ -160,11 +175,15 @@ def tile_scaleddotproductattention_t_kernel(tc, query_in, key_in, value_in, out)
                 out=osb[b][:, i, :], in0=o_ps[n][:], scalar=rc[n][:], in1=mean[b][:],
                 op0=ALU.mult, op1=ALU.subtract,
             )
-
-        def store(b, i0, i1):
-            nc.sync.dma_start(
-                out=out[b].rearrange("(p i) d -> p i d", i=4)[:, i0:i1, :], in_=osb[b][:, i0:i1, :]
-            )
+            if b < B - 1:
+                spans = {3: (0, 4)}
+            else:
+                spans = {1: (0, 2), 2: (2, 3), 3: (3, 4)}
+            if i in spans:
+                i0, i1 = spans[i]
+                nc.sync.dma_start(
+                    out=out[b].rearrange("(p i) d -> p i d", i=4)[:, i0:i1, :], in_=osb[b][:, i0:i1, :]
+                )
 
         def vreg(b, k):
             if k == 0:
@@ -186,14 +205,14 @@ def tile_scaleddotproductattention_t_kernel(tc, query_in, key_in, value_in, out)
                 in_=vg[b][:, cols, :].rearrange("p d t -> p (d t)"),
             )
 
-        def jsum(b, k):
+        def jsum(b, k, eng):
             if k == 0:
                 vsum[b] = vpool.tile([P, 512], F32, name="vsum%d" % b, tag="vsum")
             cols = slice(128 * k, 128 * k + 128)
             pk = vpool.tile([P, 128, 2], F32, name="p1_%d_%d" % (b, k), tag="p1")
             v4 = vg[b][:, cols, :].rearrange("p d (a w) -> p d a w", w=2)
-            nc.gpsimd.tensor_tensor(out=pk[:], in0=v4[:, :, :, 0], in1=v4[:, :, :, 1], op=ALU.add)
-            nc.gpsimd.tensor_tensor(out=vsum[b][:, cols], in0=pk[:, :, 0], in1=pk[:, :, 1], op=ALU.add)
+            eng.tensor_tensor(out=pk[:], in0=v4[:, :, :, 0], in1=v4[:, :, :, 1], op=ALU.add)
+            eng.tensor_tensor(out=vsum[b][:, cols], in0=pk[:, :, 0], in1=pk[:, :, 1], op=ALU.add)
 
         def meanmm(b):
             m_ps[b] = ps_m.tile([P, 512], F32, name="m%d" % b, tag="m")
@@ -204,82 +223,63 @@ def tile_scaleddotproductattention_t_kernel(tc, query_in, key_in, value_in, out)
             nc.scalar.copy(out=mean[b][:], in_=m_ps[b][:])
 
         for g4 in range(4):
-            for i in range(4):
-                pt(g4, i)
+            for x in range(4):
+                pt(g4, x)
             tcopy(g4, g4 % 2)
-        vreg(0, 0)
-        vreg(0, 1)
-        vq(0, 0)
-        jsum(0, 0)
-        jsum(0, 1)
+        for k in range(4):
+            vreg(0, k)
 
-        mean_step = dict((4 * b + 3, b) for b in range(B - 1))
-        mean_step[4 * B - 2] = B - 1
+        mean_step = dict((4 * b + 2, b) for b in range(1, B))
+        mean_step[3] = 0
+        pt_groups = {0: [4, 5], 1: [6, 7], 2: []}
+        tc_groups = {0: [], 1: [4, 5], 2: [6], 3: [7]}
         for n in range(NT + 4):
             ets = [(0, n - 2, t) for t in range(4)] if 0 <= n - 2 < NT else []
-            if n == 0:
-                groups = [4]
-            elif n == 1:
-                groups = [5, 6]
-            elif n + 5 < NT:
-                groups = [n + 5]
+            groups = pt_groups.get(n, [n + 5] if n + 5 < NT else [])
+            pts = [(1, g4, x) for g4 in groups for x in range(4)]
+            if n < 2:
+                gaps = [[], [], [], pts]
+            elif pts:
+                gaps = [pts[0:2], pts[2:4] + ets[0:1], ets[1:4], []]
             else:
-                groups = []
-            pts = [(1, g4, i) for g4 in groups for i in range(4)]
-            if n < NT:
-                if n == 0:
-                    gaps = [[], pts[0:2], pts[2:4]]
-                elif n == 1:
-                    gaps = [pts[0:3], pts[3:6], pts[6:8]]
-                else:
-                    gaps = [pts[0:2], pts[2:4] + ets[0:1], ets[1:4]]
-                for j in range(4):
+                gaps = [[], ets[0:1], ets[1:4], []]
+            for j in range(4):
+                if n < NT:
                     mm(n, j)
-                    if j < 3:
-                        for kind, a, x in gaps[j]:
-                            if kind == 0:
-                                et(a, x)
-                            else:
-                                pt(a, x)
-            else:
-                for kind, a, x in ets:
-                    et(a, x)
+                for kind, a, x in gaps[j]:
+                    if kind == 0:
+                        et(a, x)
+                    else:
+                        pt(a, x)
             if n in mean_step:
                 meanmm(mean_step[n])
             if 0 <= n - 1 < NT:
                 maxs(n - 1)
+            if n == 1:
+                for k in range(4):
+                    vq(0, k)
+                jsum(0, 0, nc.vector)
+                jsum(0, 1, nc.vector)
+            if n == 2:
+                jsum(0, 2, nc.vector)
+                jsum(0, 3, nc.vector)
+            g2 = n + 2
+            if 4 <= g2 < NT:
+                vreg(g2 // 4, g2 % 4)
+                jsum(g2 // 4, g2 % 4, nc.gpsimd)
+            if 4 <= g2 - 1 < NT:
+                vq((g2 - 1) // 4, (g2 - 1) % 4)
             if 0 <= n - 3 < NT:
                 ecopy(n - 3)
                 eq(n - 3)
-            g2 = n + 2
-            if g2 < NT:
-                vreg(g2 // 4, g2 % 4)
-            if g2 - 1 < NT:
-                vq((g2 - 1) // 4, (g2 - 1) % 4)
-            if g2 < NT:
-                jsum(g2 // 4, g2 % 4)
-            if 0 <= n - 3 < NT:
                 mx(n - 3)
+            for g4 in tc_groups.get(n, [n + 4] if n + 4 < NT else []):
+                tcopy(g4, 0)
             if n - 1 in mean_step:
                 meancopy(mean_step[n - 1])
-            if 0 <= n - 4 < NT:
-                fin(n - 4)
-                b4, i4 = divmod(n - 4, 4)
-                if b4 < B - 1:
-                    if i4 == 3:
-                        store(b4, 0, 4)
-                elif i4 == 1:
-                    store(b4, 0, 2)
-                elif i4 >= 2:
-                    store(b4, i4, i4 + 1)
-            if 0 <= n - 2 < NT:
-                recip(n - 2)
-            if n == 1:
-                tcopy(4, 0)
-            elif n == 2:
-                tcopy(5, 0)
-                tcopy(6, 0)
-            elif n >= 3 and n + 4 < NT:
-                tcopy(n + 4, 0)
             if 0 <= n - 1 < NT:
                 expo(n - 1)
+            if 0 <= n - 4 < NT:
+                fin(n - 4)
+            if 0 <= n - 2 < NT:
+                recip(n - 2)

@@ -125,10 +125,11 @@ def tile_scaleddotproductattention_t_kernel(tc, query_in, key_in, value_in, out)
 
         def expo(n):
             e_sb[n] = work.tile([P, 512], BF16, name="e%d" % n, tag="e")
-            rs[n] = small.tile([P, 1], F32, name="rs%d" % n, tag="rs")
+            if n % 2 == 0:
+                rs[n // 2] = small.tile([P, 2], F32, name="rs%d" % n, tag="rs")
             nc.scalar.activation(
                 out=e_sb[n][:], in_=sc[n][:], func=ACT.Exp, bias=nb[n][:], scale=-1.0,
-                accum_out=rs[n][:],
+                accum_out=rs[n // 2][:, n % 2 : n % 2 + 1],
             )
 
         def et(n, t):
@@ -153,9 +154,9 @@ def tile_scaleddotproductattention_t_kernel(tc, query_in, key_in, value_in, out)
                 in_=eg[n][:].rearrange("p q t -> p (q t)"),
             )
 
-        def recip(n):
-            rc[n] = small.tile([P, 1], F32, name="rc%d" % n, tag="rc")
-            nc.vector.reciprocal(out=rc[n][:], in_=rs[n][:])
+        def recip(pair):
+            rc[pair] = small.tile([P, 2], F32, name="rc%d" % pair, tag="rc")
+            nc.vector.reciprocal(out=rc[pair][:], in_=rs[pair][:])
 
         def mx(n):
             b = n // 4
@@ -172,7 +173,7 @@ def tile_scaleddotproductattention_t_kernel(tc, query_in, key_in, value_in, out)
             if i == 0:
                 osb[b] = opool.tile([P, 4, 512], F32, name="osb%d" % b, tag="osb")
             nc.vector.scalar_tensor_tensor(
-                out=osb[b][:, i, :], in0=o_ps[n][:], scalar=rc[n][:], in1=mean[b][:],
+                out=osb[b][:, i, :], in0=o_ps[n][:], scalar=rc[n // 2][:, n % 2 : n % 2 + 1], in1=mean[b][:],
                 op0=ALU.mult, op1=ALU.subtract,
             )
             if b < B - 1:
@@ -195,14 +196,12 @@ def tile_scaleddotproductattention_t_kernel(tc, query_in, key_in, value_in, out)
                 in_=src.rearrange("p t (c i) -> p c t i", i=4),
             )
 
-        def vq(b, k):
-            if k == 0:
-                vc[b] = vkeep.tile([P, 512], U32, name="vc%d" % b, tag="vc", align_bytes=64)
-                vs[b] = vkeep.tile([P, 512], U8, name="vs%d" % b, tag="vs", align_bytes=64)
-            cols = slice(128 * k, 128 * k + 128)
+        def vq(b):
+            vc[b] = vkeep.tile([P, 512], U32, name="vc%d" % b, tag="vc", align_bytes=64)
+            vs[b] = vkeep.tile([P, 512], U8, name="vs%d" % b, tag="vs", align_bytes=64)
             nc.vector.quantize_mx(
-                out=vc[b][:, cols].bitcast(FP8X4), scales=vs[b][:, cols],
-                in_=vg[b][:, cols, :].rearrange("p d t -> p (d t)"),
+                out=vc[b][:].bitcast(FP8X4), scales=vs[b][:],
+                in_=vg[b][:].rearrange("p d t -> p (d t)"),
             )
 
         def jsum(b, k, eng):
@@ -222,10 +221,18 @@ def tile_scaleddotproductattention_t_kernel(tc, query_in, key_in, value_in, out)
             mean[b] = vkeep.tile([P, 512], F32, name="mean%d" % b, tag="mean")
             nc.scalar.copy(out=mean[b][:], in_=m_ps[b][:])
 
+        warm_ps = ps_m.tile([P, P], F32, name="warm_ps", tag="m")
+
+        def keep_clock(count):
+            for rep in range(count):
+                nc.tensor.matmul(out=warm_ps[:], lhsT=ones[:], rhs=ones[:], start=True, stop=True)
+
+        keep_clock(6)
         for g4 in range(4):
             for x in range(4):
                 pt(g4, x)
             tcopy(g4, g4 % 2)
+            keep_clock((0, 2, 0, 3)[g4])
         for k in range(4):
             vreg(0, k)
 
@@ -256,8 +263,7 @@ def tile_scaleddotproductattention_t_kernel(tc, query_in, key_in, value_in, out)
             if 0 <= n - 1 < NT:
                 maxs(n - 1)
             if n == 1:
-                for k in range(4):
-                    vq(0, k)
+                vq(0)
                 jsum(0, 0, nc.vector)
                 jsum(0, 1, nc.vector)
             if n == 2:
@@ -267,8 +273,8 @@ def tile_scaleddotproductattention_t_kernel(tc, query_in, key_in, value_in, out)
             if 4 <= g2 < NT:
                 vreg(g2 // 4, g2 % 4)
                 jsum(g2 // 4, g2 % 4, nc.gpsimd)
-            if 4 <= g2 - 1 < NT:
-                vq((g2 - 1) // 4, (g2 - 1) % 4)
+            if 4 <= g2 - 1 < NT and (g2 - 1) % 4 == 3:
+                vq((g2 - 1) // 4)
             if 0 <= n - 3 < NT:
                 ecopy(n - 3)
                 eq(n - 3)
@@ -281,5 +287,5 @@ def tile_scaleddotproductattention_t_kernel(tc, query_in, key_in, value_in, out)
                 expo(n - 1)
             if 0 <= n - 4 < NT:
                 fin(n - 4)
-            if 0 <= n - 2 < NT:
-                recip(n - 2)
+            if 0 <= n - 3 < NT and (n - 3) % 2 == 0:
+                recip((n - 3) // 2)

@@ -125,11 +125,10 @@ def tile_scaleddotproductattention_t_kernel(tc, query_in, key_in, value_in, out)
 
         def expo(n):
             e_sb[n] = work.tile([P, 512], BF16, name="e%d" % n, tag="e")
-            if n % 2 == 0:
-                rs[n // 2] = small.tile([P, 2], F32, name="rs%d" % n, tag="rs")
+            rs[n] = small.tile([P, 1], F32, name="rs%d" % n, tag="rs")
             nc.scalar.activation(
                 out=e_sb[n][:], in_=sc[n][:], func=ACT.Exp, bias=nb[n][:], scale=-1.0,
-                accum_out=rs[n // 2][:, n % 2 : n % 2 + 1],
+                accum_out=rs[n][:],
             )
 
         def et(n, t):
@@ -154,9 +153,9 @@ def tile_scaleddotproductattention_t_kernel(tc, query_in, key_in, value_in, out)
                 in_=eg[n][:].rearrange("p q t -> p (q t)"),
             )
 
-        def recip(pair):
-            rc[pair] = small.tile([P, 2], F32, name="rc%d" % pair, tag="rc")
-            nc.vector.reciprocal(out=rc[pair][:], in_=rs[pair][:])
+        def recip(n):
+            rc[n] = small.tile([P, 1], F32, name="rc%d" % n, tag="rc")
+            nc.vector.reciprocal(out=rc[n][:], in_=rs[n][:])
 
         def mx(n):
             b = n // 4
@@ -173,7 +172,7 @@ def tile_scaleddotproductattention_t_kernel(tc, query_in, key_in, value_in, out)
             if i == 0:
                 osb[b] = opool.tile([P, 4, 512], F32, name="osb%d" % b, tag="osb")
             nc.vector.scalar_tensor_tensor(
-                out=osb[b][:, i, :], in0=o_ps[n][:], scalar=rc[n // 2][:, n % 2 : n % 2 + 1], in1=mean[b][:],
+                out=osb[b][:, i, :], in0=o_ps[n][:], scalar=rc[n][:], in1=mean[b][:],
                 op0=ALU.mult, op1=ALU.subtract,
             )
             if b < B - 1:
@@ -196,12 +195,14 @@ def tile_scaleddotproductattention_t_kernel(tc, query_in, key_in, value_in, out)
                 in_=src.rearrange("p t (c i) -> p c t i", i=4),
             )
 
-        def vq(b):
-            vc[b] = vkeep.tile([P, 512], U32, name="vc%d" % b, tag="vc", align_bytes=64)
-            vs[b] = vkeep.tile([P, 512], U8, name="vs%d" % b, tag="vs", align_bytes=64)
+        def vq(b, k):
+            if k == 0:
+                vc[b] = vkeep.tile([P, 512], U32, name="vc%d" % b, tag="vc", align_bytes=64)
+                vs[b] = vkeep.tile([P, 512], U8, name="vs%d" % b, tag="vs", align_bytes=64)
+            cols = slice(128 * k, 128 * k + 128)
             nc.vector.quantize_mx(
-                out=vc[b][:].bitcast(FP8X4), scales=vs[b][:],
-                in_=vg[b][:].rearrange("p d t -> p (d t)"),
+                out=vc[b][:, cols].bitcast(FP8X4), scales=vs[b][:, cols],
+                in_=vg[b][:, cols, :].rearrange("p d t -> p (d t)"),
             )
 
         def jsum(b, k, eng):
@@ -213,31 +214,29 @@ def tile_scaleddotproductattention_t_kernel(tc, query_in, key_in, value_in, out)
             eng.tensor_tensor(out=pk[:], in0=v4[:, :, :, 0], in1=v4[:, :, :, 1], op=ALU.add)
             eng.tensor_tensor(out=vsum[b][:, cols], in0=pk[:, :, 0], in1=pk[:, :, 1], op=ALU.add)
 
-        def meanmm(b):
-            m_ps[b] = ps_m.tile([P, 512], F32, name="m%d" % b, tag="m")
-            nc.tensor.matmul(out=m_ps[b][:], lhsT=ones[:], rhs=vsum[b][:], start=True, stop=True)
+        def meanmm(b, k0, k1):
+            if k0 == 0:
+                m_ps[b] = ps_m.tile([P, 512], F32, name="m%d" % b, tag="m")
+            cols = slice(128 * k0, 128 * k1)
+            nc.tensor.matmul(
+                out=m_ps[b][:, cols], lhsT=ones[:], rhs=vsum[b][:, cols], start=True, stop=True
+            )
 
-        def meancopy(b):
-            mean[b] = vkeep.tile([P, 512], F32, name="mean%d" % b, tag="mean")
-            nc.scalar.copy(out=mean[b][:], in_=m_ps[b][:])
+        def meancopy(b, k0, k1):
+            if k0 == 0:
+                mean[b] = vkeep.tile([P, 512], F32, name="mean%d" % b, tag="mean")
+            cols = slice(128 * k0, 128 * k1)
+            nc.scalar.copy(out=mean[b][:, cols], in_=m_ps[b][:, cols])
 
-        warm_ps = ps_m.tile([P, P], F32, name="warm_ps", tag="m")
-
-        def keep_clock(count):
-            for rep in range(count):
-                nc.tensor.matmul(out=warm_ps[:], lhsT=ones[:], rhs=ones[:], start=True, stop=True)
-
-        keep_clock(6)
         for g4 in range(4):
             for x in range(4):
                 pt(g4, x)
             tcopy(g4, g4 % 2)
-            keep_clock((0, 2, 0, 3)[g4])
         for k in range(4):
             vreg(0, k)
 
-        mean_step = dict((4 * b + 2, b) for b in range(1, B))
-        mean_step[3] = 0
+        mean_step = dict((n, (n // 4, n % 4, n % 4 + 1)) for n in range(4, NT))
+        mean_step[3] = (0, 0, 4)
         pt_groups = {0: [4, 5], 1: [6, 7], 2: []}
         tc_groups = {0: [], 1: [4, 5], 2: [6], 3: [7]}
         for n in range(NT + 4):
@@ -259,11 +258,12 @@ def tile_scaleddotproductattention_t_kernel(tc, query_in, key_in, value_in, out)
                     else:
                         pt(a, x)
             if n in mean_step:
-                meanmm(mean_step[n])
+                meanmm(*mean_step[n])
             if 0 <= n - 1 < NT:
                 maxs(n - 1)
             if n == 1:
-                vq(0)
+                for k in range(4):
+                    vq(0, k)
                 jsum(0, 0, nc.vector)
                 jsum(0, 1, nc.vector)
             if n == 2:
@@ -273,8 +273,8 @@ def tile_scaleddotproductattention_t_kernel(tc, query_in, key_in, value_in, out)
             if 4 <= g2 < NT:
                 vreg(g2 // 4, g2 % 4)
                 jsum(g2 // 4, g2 % 4, nc.gpsimd)
-            if 4 <= g2 - 1 < NT and (g2 - 1) % 4 == 3:
-                vq((g2 - 1) // 4)
+            if 4 <= g2 - 1 < NT:
+                vq((g2 - 1) // 4, (g2 - 1) % 4)
             if 0 <= n - 3 < NT:
                 ecopy(n - 3)
                 eq(n - 3)
@@ -282,10 +282,10 @@ def tile_scaleddotproductattention_t_kernel(tc, query_in, key_in, value_in, out)
             for g4 in tc_groups.get(n, [n + 4] if n + 4 < NT else []):
                 tcopy(g4, 0)
             if n - 1 in mean_step:
-                meancopy(mean_step[n - 1])
+                meancopy(*mean_step[n - 1])
             if 0 <= n - 1 < NT:
                 expo(n - 1)
             if 0 <= n - 4 < NT:
                 fin(n - 4)
-            if 0 <= n - 3 < NT and (n - 3) % 2 == 0:
-                recip((n - 3) // 2)
+            if 0 <= n - 2 < NT:
+                recip(n - 2)

@@ -222,11 +222,9 @@ def tile_scaleddotproductattention_t_kernel(tc, query_in, key_in, value_in, out)
                 out=m_ps[b][:, cols], lhsT=ones[:], rhs=vsum[b][:, cols], start=True, stop=True
             )
 
-        def meancopy(b, k0, k1):
-            if k0 == 0:
-                mean[b] = vkeep.tile([P, 512], F32, name="mean%d" % b, tag="mean")
-            cols = slice(128 * k0, 128 * k1)
-            nc.scalar.copy(out=mean[b][:, cols], in_=m_ps[b][:, cols])
+        def meancopy(b):
+            mean[b] = vkeep.tile([P, 512], F32, name="mean%d" % b, tag="mean")
+            nc.scalar.copy(out=mean[b][:], in_=m_ps[b][:])
 
         for g4 in range(4):
             for x in range(4):
@@ -235,8 +233,10 @@ def tile_scaleddotproductattention_t_kernel(tc, query_in, key_in, value_in, out)
         for k in range(4):
             vreg(0, k)
 
-        mean_step = dict((n, (n // 4, n % 4, n % 4 + 1)) for n in range(4, NT))
-        mean_step[3] = (0, 0, 4)
+        mean_step = {3: (0, 0, 4)}
+        for b in range(1, B):
+            mean_step[4 * b + 1] = (b, 0, 2)
+            mean_step[4 * b + 2] = (b, 2, 4)
         pt_groups = {0: [4, 5], 1: [6, 7], 2: []}
         tc_groups = {0: [], 1: [4, 5], 2: [6], 3: [7]}
         for n in range(NT + 4):
@@ -281,8 +281,8 @@ def tile_scaleddotproductattention_t_kernel(tc, query_in, key_in, value_in, out)
                 mx(n - 3)
             for g4 in tc_groups.get(n, [n + 4] if n + 4 < NT else []):
                 tcopy(g4, 0)
-            if n - 1 in mean_step:
-                meancopy(*mean_step[n - 1])
+            if n - 1 in mean_step and mean_step[n - 1][2] == 4:
+                meancopy(mean_step[n - 1][0])
             if 0 <= n - 1 < NT:
                 expo(n - 1)
             if 0 <= n - 4 < NT:

@@ -39,8 +39,6 @@ def tile_scaleddotproductattention_t_kernel(tc, query_in, key_in, value_in, out)
 
         ident_f = const.tile([P, P], F32, name="ident_f")
         make_identity(nc, ident_f[:])
-        ident_b = const.tile([P, P], BF16, name="ident_b")
-        make_identity(nc, ident_b[:])
         ones = const.tile([P, P], F32, name="ones")
         nc.vector.memset(ones[:], 1.0 / T)
         warm = const.tile([P, 1], F32, name="warm")
@@ -95,6 +93,9 @@ def tile_scaleddotproductattention_t_kernel(tc, query_in, key_in, value_in, out)
             words = qkt[(nm, b)][:].bitcast(F32).rearrange("p (u c) -> p u c", u=2)
             dst = words[:, :, 256 * h : 256 * h + 256]
             src = tp[g4][:].rearrange("p (u c) -> p u c", u=2)
+            if nm == "k":
+                dst = dst.rearrange("p u (c i) -> p u c i", i=2)
+                src = tp[g4][:].rearrange("p (u i c) -> p u c i", u=2, i=2)
             if eng == 0:
                 nc.scalar.copy(out=dst, in_=src)
             else:
@@ -134,16 +135,20 @@ def tile_scaleddotproductattention_t_kernel(tc, query_in, key_in, value_in, out)
         def et(n, t):
             if t == 0:
                 if n >= NT - 5 and n % 2 == 1:
-                    et_ps[n] = ps_t.tile([P, 4, P], BF16, name="et%d" % n, tag="tp")
+                    et_ps[n] = ps_t.tile([P, 2, P], F32, name="et%d" % n, tag="tp")
                 else:
-                    et_ps[n] = ps_e.tile([P, 4, P], BF16, name="et%d" % n, tag="et")
+                    et_ps[n] = ps_e.tile([P, 2, P], F32, name="et%d" % n, tag="et")
             nc.tensor.transpose(
-                out=et_ps[n][:, t, :], in_=e_sb[n][:, 128 * t : 128 * t + 128], identity=ident_b[:]
+                out=et_ps[n][:, t, :], in_=e_sb[n][:].bitcast(F32)[:, 128 * t : 128 * t + 128],
+                identity=ident_f[:],
             )
 
         def ecopy(n):
             eg[n] = work.tile([P, P, 4], BF16, name="eg%d" % n, tag="eg", align_bytes=64)
-            nc.scalar.copy(out=eg[n][:], in_=et_ps[n][:].rearrange("p t q -> p q t"))
+            nc.scalar.copy(
+                out=eg[n][:].rearrange("p q t -> p (q t)").bitcast(F32).rearrange("p (q h) -> p q h", h=2),
+                in_=et_ps[n][:].rearrange("p h q -> p q h"),
+            )
 
         def eq(n):
             ec[n] = work.tile([P, P], U32, name="ec%d" % n, tag="ec", align_bytes=64)
@@ -240,15 +245,15 @@ def tile_scaleddotproductattention_t_kernel(tc, query_in, key_in, value_in, out)
         pt_groups = {0: [4, 5], 1: [6, 7], 2: []}
         tc_groups = {0: [], 1: [4, 5], 2: [6], 3: [7]}
         for n in range(NT + 4):
-            ets = [(0, n - 2, t) for t in range(4)] if 0 <= n - 2 < NT else []
+            ets = [(0, n - 2, t) for t in range(2)] if 0 <= n - 2 < NT else []
             groups = pt_groups.get(n, [n + 5] if n + 5 < NT else [])
             pts = [(1, g4, x) for g4 in groups for x in range(4)]
             if n < 2:
                 gaps = [[], [], [], pts]
             elif pts:
-                gaps = [pts[0:2], pts[2:4] + ets[0:1], ets[1:4], []]
+                gaps = [pts[0:2], pts[2:4] + ets[0:1], ets[1:2], []]
             else:
-                gaps = [[], ets[0:1], ets[1:4], []]
+                gaps = [[], ets[0:1], ets[1:2], []]
             for j in range(4):
                 if n < NT:
                     mm(n, j)

@@ -17,6 +17,7 @@ FP8X4 = mybir.dt.float8_e4m3fn_x4
 ALU = mybir.AluOpType
 ACT = mybir.ActivationFunctionType
 SCALE = 1.0 / math.sqrt(D)
+VSPLIT = 64
 
 
 def tile_scaleddotproductattention_t_kernel(tc, query_in, key_in, value_in, out):
@@ -190,15 +191,21 @@ def tile_scaleddotproductattention_t_kernel(tc, query_in, key_in, value_in, out)
                     out=out[b].rearrange("(p i) d -> p i d", i=4)[:, i0:i1, :], in_=osb[b][:, i0:i1, :]
                 )
 
-        def vreg(b, k):
-            if k == 0:
+        def vreg(b, k, c0=0, c1=128, eng=1):
+            if k == 0 and c0 == 0:
                 vg[b] = vpool.tile([P, 512, 4], BF16, name="vg%d" % b, tag="vg", align_bytes=64)
-            dst = vg[b][:, 128 * k : 128 * k + 128, :]
-            src = v_sb[b][:].rearrange("p (t d) -> p t d", t=4)[:, :, 128 * k : 128 * k + 128]
-            nc.vector.tensor_copy(
-                out=dst.rearrange("p (c i) t -> p c t i", i=4),
-                in_=src.rearrange("p t (c i) -> p c t i", i=4),
-            )
+            dst = vg[b][:, 128 * k + c0 : 128 * k + c1, :]
+            src = v_sb[b][:].rearrange("p (t d) -> p t d", t=4)[:, :, 128 * k + c0 : 128 * k + c1]
+            if eng == 0:
+                nc.scalar.copy(
+                    out=dst.rearrange("p (c i) t -> p c t i", i=4),
+                    in_=src.rearrange("p t (c i) -> p c t i", i=4),
+                )
+            else:
+                nc.vector.tensor_copy(
+                    out=dst.rearrange("p (c i) t -> p c t i", i=4),
+                    in_=src.rearrange("p t (c i) -> p c t i", i=4),
+                )
 
         def vq(b, k):
             if k == 0:
@@ -276,8 +283,7 @@ def tile_scaleddotproductattention_t_kernel(tc, query_in, key_in, value_in, out)
                 jsum(0, 3, nc.vector)
             g2 = n + 2
             if 4 <= g2 < NT:
-                vreg(g2 // 4, g2 % 4)
-                jsum(g2 // 4, g2 % 4, nc.gpsimd)
+                vreg(g2 // 4, g2 % 4, 0, VSPLIT, 1)
             if 4 <= g2 - 1 < NT:
                 vq((g2 - 1) // 4, (g2 - 1) % 4)
             if 0 <= n - 3 < NT:
@@ -286,6 +292,9 @@ def tile_scaleddotproductattention_t_kernel(tc, query_in, key_in, value_in, out)
                 mx(n - 3)
             for g4 in tc_groups.get(n, [n + 4] if n + 4 < NT else []):
                 tcopy(g4, 0)
+            if 4 <= g2 < NT:
+                vreg(g2 // 4, g2 % 4, VSPLIT, 128, 0)
+                jsum(g2 // 4, g2 % 4, nc.gpsimd)
             if n - 1 in mean_step and mean_step[n - 1][2] == 4:
                 meancopy(mean_step[n - 1][0])
             if 0 <= n - 1 < NT:

@@ -282,8 +282,9 @@ def tile_scaleddotproductattention_t_kernel(tc, query_in, key_in, value_in, out)
                 jsum(0, 2, nc.vector)
                 jsum(0, 3, nc.vector)
             g2 = n + 2
+            vsplit = 128 if (n - 1 in mean_step and mean_step[n - 1][2] == 4) else VSPLIT
             if 4 <= g2 < NT:
-                vreg(g2 // 4, g2 % 4, 0, VSPLIT, 1)
+                vreg(g2 // 4, g2 % 4, 0, vsplit, 1)
             if 4 <= g2 - 1 < NT:
                 vq((g2 - 1) // 4, (g2 - 1) % 4)
             if 0 <= n - 3 < NT:
@@ -293,7 +294,8 @@ def tile_scaleddotproductattention_t_kernel(tc, query_in, key_in, value_in, out)
             for g4 in tc_groups.get(n, [n + 4] if n + 4 < NT else []):
                 tcopy(g4, 0)
             if 4 <= g2 < NT:
-                vreg(g2 // 4, g2 % 4, VSPLIT, 128, 0)
+                if vsplit < 128:
+                    vreg(g2 // 4, g2 % 4, vsplit, 128, 0)
                 jsum(g2 // 4, g2 % 4, nc.gpsimd)
             if n - 1 in mean_step and mean_step[n - 1][2] == 4:
                 meancopy(mean_step[n - 1][0])

@@ -16,6 +16,9 @@ U8 = mybir.dt.uint8
 FP8X4 = mybir.dt.float8_e4m3fn_x4
 ALU = mybir.AluOpType
 ACT = mybir.ActivationFunctionType
+AX = mybir.AxisListType
+GP = 4
+NG = P // GP
 SCALE = 1.0 / math.sqrt(D)
 VSPLIT = 64
 
@@ -40,8 +43,12 @@ def tile_scaleddotproductattention_t_kernel(tc, query_in, key_in, value_in, out)
 
         ident_f = const.tile([P, P], F32, name="ident_f")
         make_identity(nc, ident_f[:])
-        ones = const.tile([P, P], F32, name="ones")
-        nc.vector.memset(ones[:], 1.0 / T)
+        sel_f = const.tile([P, NG], F32, name="sel_f")
+        nc.vector.tensor_reduce(
+            out=sel_f[:], in_=ident_f[:].rearrange("p (g j) -> p g j", j=GP), axis=AX.X, op=ALU.add
+        )
+        sel = const.tile([P, NG], BF16, name="sel")
+        nc.vector.tensor_scalar(out=sel[:], in0=sel_f[:], scalar1=1.0 / T, scalar2=None, op0=ALU.mult)
         warm = const.tile([P, 1], F32, name="warm")
         nc.vector.memset(warm[:], 0.0)
         warm2 = const.tile([P, 1], F32, name="warm2")
@@ -68,7 +75,7 @@ def tile_scaleddotproductattention_t_kernel(tc, query_in, key_in, value_in, out)
 
         qkt, tp = {}, {}
         s_ps, sc, nb, rs, rc, e_sb, et_ps, eg, ec, es, o_ps = {}, {}, {}, {}, {}, {}, {}, {}, {}, {}, {}
-        vg, vc, vs, vsum, m_ps, mean, osb = {}, {}, {}, {}, {}, {}, {}
+        vg, vc, vs, mcol, m_ps, mean, osb = {}, {}, {}, {}, {}, {}, {}
 
         def group(g4):
             b, g = divmod(g4, 4)
@@ -217,21 +224,27 @@ def tile_scaleddotproductattention_t_kernel(tc, query_in, key_in, value_in, out)
                 in_=vg[b][:, cols, :].rearrange("p d t -> p (d t)"),
             )
 
-        def jsum(b, k, eng):
-            if k == 0:
-                vsum[b] = vpool.tile([P, 512], F32, name="vsum%d" % b, tag="vsum")
-            cols = slice(128 * k, 128 * k + 128)
-            pk = vpool.tile([P, 128, 2], F32, name="p1_%d_%d" % (b, k), tag="p1")
-            v4 = vg[b][:, cols, :].rearrange("p d (a w) -> p d a w", w=2)
-            eng.tensor_tensor(out=pk[:], in0=v4[:, :, :, 0], in1=v4[:, :, :, 1], op=ALU.add)
-            eng.tensor_tensor(out=vsum[b][:, cols], in0=pk[:, :, 0], in1=pk[:, :, 1], op=ALU.add)
-
-        def meanmm(b, k0, k1):
-            if k0 == 0:
+        def msum(b, c):
+            if c == 0:
                 m_ps[b] = ps_m.tile([P, 512], F32, name="m%d" % b, tag="m")
-            cols = slice(128 * k0, 128 * k1)
-            nc.tensor.matmul(
-                out=m_ps[b][:, cols], lhsT=ones[:], rhs=vsum[b][:, cols], start=True, stop=True
+            for t in range(4):
+                col = 512 * t + 128 * c
+                nc.tensor.matmul(
+                    out=m_ps[b][:, NG * c : NG * c + NG], lhsT=v_sb[b][:, col : col + 128], rhs=sel[:],
+                    start=(t == 0), stop=(t == 3),
+                )
+
+        def mred(b):
+            mcol[b] = small.tile([P, 4], F32, name="mcol%d" % b, tag="mcol")
+            nc.vector.tensor_reduce(
+                out=mcol[b][:], in_=m_ps[b][:, 0 : 4 * NG].rearrange("p (c g) -> p c g", g=NG),
+                axis=AX.X, op=ALU.add,
+            )
+
+        def mbc(b, c):
+            nc.tensor.transpose(
+                out=m_ps[b][:, 128 * c : 128 * c + 128], in_=mcol[b][:, c : c + 1].to_broadcast([P, P]),
+                identity=ident_f[:],
             )
 
         def meancopy(b):
@@ -245,10 +258,6 @@ def tile_scaleddotproductattention_t_kernel(tc, query_in, key_in, value_in, out)
         for k in range(4):
             vreg(0, k)
 
-        mean_step = {3: (0, 0, 4)}
-        for b in range(1, B):
-            mean_step[4 * b + 1] = (b, 0, 2)
-            mean_step[4 * b + 2] = (b, 2, 4)
         pt_groups = {0: [4, 5], 1: [6, 7], 2: []}
         tc_groups = {0: [], 1: [4, 5], 2: [6], 3: [7]}
         for n in range(NT + 4):
@@ -261,6 +270,11 @@ def tile_scaleddotproductattention_t_kernel(tc, query_in, key_in, value_in, out)
                 gaps = [pts[0:2], pts[2:4] + ets[0:1], ets[1:2], []]
             else:
                 gaps = [[], ets[0:1], ets[1:2], []]
+            bm, ph = divmod(n, 4)
+            if 0 <= n - 1 < NT:
+                maxs(n - 1)
+            if ph == 2 and n < NT:
+                mred(bm)
             for j in range(4):
                 if n < NT:
                     mm(n, j)
@@ -269,20 +283,17 @@ def tile_scaleddotproductattention_t_kernel(tc, query_in, key_in, value_in, out)
                         et(a, x)
                     else:
                         pt(a, x)
-            if n in mean_step:
-                meanmm(*mean_step[n])
-            if 0 <= n - 1 < NT:
-                maxs(n - 1)
+                if j == 2 and ph == 2 and n < NT:
+                    for c in range(4):
+                        mbc(bm, c)
+            if ph < 2 and n < NT:
+                msum(bm, 2 * ph)
+                msum(bm, 2 * ph + 1)
             if n == 1:
                 for k in range(4):
                     vq(0, k)
-                jsum(0, 0, nc.vector)
-                jsum(0, 1, nc.vector)
-            if n == 2:
-                jsum(0, 2, nc.vector)
-                jsum(0, 3, nc.vector)
             g2 = n + 2
-            vsplit = 128 if (n - 1 in mean_step and mean_step[n - 1][2] == 4) else VSPLIT
+            vsplit = 128 if ph == 3 else VSPLIT
             if 4 <= g2 < NT:
                 vreg(g2 // 4, g2 % 4, 0, vsplit, 1)
             if 4 <= g2 - 1 < NT:
@@ -296,9 +307,8 @@ def tile_scaleddotproductattention_t_kernel(tc, query_in, key_in, value_in, out)
             if 4 <= g2 < NT:
                 if vsplit < 128:
                     vreg(g2 // 4, g2 % 4, vsplit, 128, 0)
-                jsum(g2 // 4, g2 % 4, nc.gpsimd)
-            if n - 1 in mean_step and mean_step[n - 1][2] == 4:
-                meancopy(mean_step[n - 1][0])
+            if ph == 3 and n < NT:
+                meancopy(bm)
             if 0 <= n - 1 < NT:
                 expo(n - 1)
             if 0 <= n - 4 < NT:

@@ -20,7 +20,6 @@ AX = mybir.AxisListType
 GP = 4
 NG = P // GP
 SCALE = 1.0 / math.sqrt(D)
-VSPLIT = 64
 
 
 def tile_scaleddotproductattention_t_kernel(tc, query_in, key_in, value_in, out):
@@ -31,7 +30,7 @@ def tile_scaleddotproductattention_t_kernel(tc, query_in, key_in, value_in, out)
         trp = ctx.enter_context(tc.tile_pool(name="trp", bufs=2))
         work = ctx.enter_context(tc.tile_pool(name="work", bufs=3))
         small = ctx.enter_context(tc.tile_pool(name="small", bufs=6))
-        vpool = ctx.enter_context(tc.tile_pool(name="vpool", bufs=2))
+        vpool = ctx.enter_context(tc.tile_pool(name="vpool", bufs=4))
         vkeep = ctx.enter_context(tc.tile_pool(name="vkeep", bufs=3))
         opool = ctx.enter_context(tc.tile_pool(name="opool", bufs=3))
         ps_s = ctx.enter_context(tc.psum_pool(name="ps_s", bufs=2))
@@ -198,20 +197,18 @@ def tile_scaleddotproductattention_t_kernel(tc, query_in, key_in, value_in, out)
                     out=out[b].rearrange("(p i) d -> p i d", i=4)[:, i0:i1, :], in_=osb[b][:, i0:i1, :]
                 )
 
-        def vreg(b, k, c0=0, c1=128, eng=1):
-            if k == 0 and c0 == 0:
-                vg[b] = vpool.tile([P, 512, 4], BF16, name="vg%d" % b, tag="vg", align_bytes=64)
-            dst = vg[b][:, 128 * k + c0 : 128 * k + c1, :]
-            src = v_sb[b][:].rearrange("p (t d) -> p t d", t=4)[:, :, 128 * k + c0 : 128 * k + c1]
-            if eng == 0:
-                nc.scalar.copy(
-                    out=dst.rearrange("p (c i) t -> p c t i", i=4),
+        def vreg(b, k, eng):
+            vg[(b, k)] = vpool.tile([P, 128, 4], BF16, name="vg%d_%d" % (b, k), tag="vg", align_bytes=64)
+            src = v_sb[b][:].rearrange("p (t d) -> p t d", t=4)[:, :, 128 * k : 128 * k + 128]
+            if eng == 1:
+                nc.vector.tensor_copy(
+                    out=vg[(b, k)][:].rearrange("p (c i) t -> p c t i", i=4),
                     in_=src.rearrange("p t (c i) -> p c t i", i=4),
                 )
             else:
-                nc.vector.tensor_copy(
-                    out=dst.rearrange("p (c i) t -> p c t i", i=4),
-                    in_=src.rearrange("p t (c i) -> p c t i", i=4),
+                nc.gpsimd.tensor_scalar(
+                    out=vg[(b, k)][:], in0=src.rearrange("p t d -> p d t"), scalar1=1.0, scalar2=0.0,
+                    op0=ALU.mult, op1=ALU.add,
                 )
 
         def vq(b, k):
@@ -221,7 +218,7 @@ def tile_scaleddotproductattention_t_kernel(tc, query_in, key_in, value_in, out)
             cols = slice(128 * k, 128 * k + 128)
             nc.vector.quantize_mx(
                 out=vc[b][:, cols].bitcast(FP8X4), scales=vs[b][:, cols],
-                in_=vg[b][:, cols, :].rearrange("p d t -> p (d t)"),
+                in_=vg[(b, k)][:].rearrange("p d t -> p (d t)"),
             )
 
         def msum(b, c):
@@ -256,7 +253,7 @@ def tile_scaleddotproductattention_t_kernel(tc, query_in, key_in, value_in, out)
                 pt(g4, x)
             tcopy(g4, g4 % 2)
         for k in range(4):
-            vreg(0, k)
+            vreg(0, k, 1)
 
         pt_groups = {0: [4, 5], 1: [6, 7], 2: []}
         tc_groups = {0: [], 1: [4, 5], 2: [6], 3: [7]}
@@ -289,24 +286,21 @@ def tile_scaleddotproductattention_t_kernel(tc, query_in, key_in, value_in, out)
             if ph < 2 and n < NT:
                 msum(bm, 2 * ph)
                 msum(bm, 2 * ph + 1)
-            if n == 1:
-                for k in range(4):
-                    vq(0, k)
-            g2 = n + 2
-            vsplit = 128 if ph == 3 else VSPLIT
-            if 4 <= g2 < NT:
-                vreg(g2 // 4, g2 % 4, 0, vsplit, 1)
-            if 4 <= g2 - 1 < NT:
-                vq((g2 - 1) // 4, (g2 - 1) % 4)
             if 0 <= n - 3 < NT:
                 ecopy(n - 3)
                 eq(n - 3)
                 mx(n - 3)
+            if n == 1:
+                for k in range(4):
+                    vq(0, k)
+                vreg(1, 0, 0)
+                vreg(1, 1, 0)
+            if 4 <= n + 1 < NT:
+                vq((n + 1) // 4, (n + 1) % 4)
+            if n >= 1 and n + 5 < NT:
+                vreg((n + 5) // 4, (n + 5) % 4, 0)
             for g4 in tc_groups.get(n, [n + 4] if n + 4 < NT else []):
                 tcopy(g4, 0)
-            if 4 <= g2 < NT:
-                if vsplit < 128:
-                    vreg(g2 // 4, g2 % 4, vsplit, 128, 0)
             if ph == 3 and n < NT:
                 meancopy(bm)
             if 0 <= n - 1 < NT:

@@ -40,6 +40,12 @@ def tile_scaleddotproductattention_t_kernel(tc, query_in, key_in, value_in, out)
         ps_m = ctx.enter_context(tc.psum_pool(name="ps_m", bufs=1))
         ctx.enter_context(tc.manual_schedule())
 
+        wz = const.tile([P, 512], BF16, name="wz")
+        nc.vector.memset(wz[:], 0.0)
+        wps = ps_o.tile([P, 512], F32, name="wps", tag="o")
+        for w in range(4):
+            nc.tensor.matmul(out=wps[:], lhsT=wz[:, 0:128], rhs=wz[:], start=True, stop=True)
+
         ident_f = const.tile([P, P], F32, name="ident_f")
         make_identity(nc, ident_f[:])
         sel_f = const.tile([P, NG], F32, name="sel_f")
@@ -263,10 +269,8 @@ def tile_scaleddotproductattention_t_kernel(tc, query_in, key_in, value_in, out)
             pts = [(1, g4, x) for g4 in groups for x in range(4)]
             if n < 2:
                 gaps = [[], [], [], pts]
-            elif pts:
-                gaps = [pts[0:2], pts[2:4] + ets[0:1], ets[1:2], []]
             else:
-                gaps = [[], ets[0:1], ets[1:2], []]
+                gaps = [[], pts[0:2], pts[2:4], ets]
             bm, ph = divmod(n, 4)
             if 0 <= n - 1 < NT:
                 maxs(n - 1)
@@ -275,12 +279,14 @@ def tile_scaleddotproductattention_t_kernel(tc, query_in, key_in, value_in, out)
             for j in range(4):
                 if n < NT:
                     mm(n, j)
+                if j == 0 and 0 <= n - 4 < NT:
+                    mx(n - 4)
                 for kind, a, x in gaps[j]:
                     if kind == 0:
                         et(a, x)
                     else:
                         pt(a, x)
-                if j == 2 and ph == 2 and n < NT:
+                if j == 3 and ph == 2 and n < NT:
                     for c in range(4):
                         mbc(bm, c)
             if ph < 2 and n < NT:
@@ -289,7 +295,6 @@ def tile_scaleddotproductattention_t_kernel(tc, query_in, key_in, value_in, out)
             if 0 <= n - 3 < NT:
                 ecopy(n - 3)
                 eq(n - 3)
-                mx(n - 3)
             if n == 1:
                 for k in range(4):
                     vq(0, k)

@@ -40,11 +40,15 @@ def tile_scaleddotproductattention_t_kernel(tc, query_in, key_in, value_in, out)
         ps_m = ctx.enter_context(tc.psum_pool(name="ps_m", bufs=1))
         ctx.enter_context(tc.manual_schedule())
 
-        wz = const.tile([P, 512], BF16, name="wz")
+        wz = const.tile([P, P], F32, name="wz")
         nc.vector.memset(wz[:], 0.0)
         wps = ps_o.tile([P, 512], F32, name="wps", tag="o")
+
+        def warm_pe(ps=wps):
+            nc.tensor.matmul(out=ps[:, 0:128], lhsT=wz[:], rhs=wz[:], start=True, stop=True)
+
         for w in range(4):
-            nc.tensor.matmul(out=wps[:], lhsT=wz[:, 0:128], rhs=wz[:], start=True, stop=True)
+            warm_pe()
 
         ident_f = const.tile([P, P], F32, name="ident_f")
         make_identity(nc, ident_f[:])
@@ -257,6 +261,7 @@ def tile_scaleddotproductattention_t_kernel(tc, query_in, key_in, value_in, out)
         for g4 in range(4):
             for x in range(4):
                 pt(g4, x)
+            warm_pe()
             tcopy(g4, g4 % 2)
         for k in range(4):
             vreg(0, k, 1)
@@ -292,6 +297,10 @@ def tile_scaleddotproductattention_t_kernel(tc, query_in, key_in, value_in, out)
             if ph < 2 and n < NT:
                 msum(bm, 2 * ph)
                 msum(bm, 2 * ph + 1)
+            if NT <= n < NT + 3:
+                if n == NT:
+                    wtail = ps_m.tile([P, 512], F32, name="wtail", tag="m")
+                warm_pe(wtail)
             if 0 <= n - 3 < NT:
                 ecopy(n - 3)
                 eq(n - 3)

@@ -42,10 +42,10 @@ def tile_scaleddotproductattention_t_kernel(tc, query_in, key_in, value_in, out)
 
         wz = const.tile([P, P], F32, name="wz")
         nc.vector.memset(wz[:], 0.0)
-        wps = ps_o.tile([P, 512], F32, name="wps", tag="o")
+        wps = ps_e.tile([P, P], F32, name="wps", tag="et")
 
         def warm_pe(ps=wps):
-            nc.tensor.matmul(out=ps[:, 0:128], lhsT=wz[:], rhs=wz[:], start=True, stop=True)
+            nc.tensor.matmul(out=ps[:, 0:P], lhsT=wz[:], rhs=wz[:], start=True, stop=True)
 
         for w in range(4):
             warm_pe()
@@ -71,9 +71,10 @@ def tile_scaleddotproductattention_t_kernel(tc, query_in, key_in, value_in, out)
             nc.sync.dma_start(out=t[:], in_=view[:, i0 * D : i1 * D])
             return t
 
-        for nm, src in (("k", key_in), ("q", query_in)):
-            for h in range(2):
-                qk_sb[(nm, 0, h)] = (load_rows(src, 0, 2 * h, 2 * h + 2, nm), 0)
+        for h in range(2):
+            qk_sb[("k", 0, h)] = (load_rows(key_in, 0, 2 * h, 2 * h + 2, "k"), 0)
+        q_first = [load_rows(query_in, 0, ii, ii + 1, "q") for ii in range(2)]
+        qk_sb[("q", 0, 1)] = (load_rows(query_in, 0, 2, 4, "q"), 0)
         v_sb[0] = load_rows(value_in, 0, 0, 4, "v")
         for b in range(1, B):
             for nm, src in (("k", key_in), ("q", query_in)):
@@ -96,7 +97,10 @@ def tile_scaleddotproductattention_t_kernel(tc, query_in, key_in, value_in, out)
             src, i0 = qk_sb[(nm, b, h)]
             col = 256 * (i0 + ii) + 128 * u
             if x == 0:
-                tp[g4] = ps_t.tile([P, 512], F32, name="tp%d" % g4, tag="tp")
+                if g4 in (6, 7):
+                    tp[g4] = ps_o.tile([P, 512], F32, name="tp%d" % g4, tag="o")
+                else:
+                    tp[g4] = ps_t.tile([P, 512], F32, name="tp%d" % g4, tag="tp")
             nc.tensor.transpose(
                 out=tp[g4][:, 128 * x : 128 * x + 128],
                 in_=src[:].bitcast(F32)[:, col : col + 128],
@@ -105,7 +109,7 @@ def tile_scaleddotproductattention_t_kernel(tc, query_in, key_in, value_in, out)
 
         def tcopy(g4, eng):
             nm, b, h = group(g4)
-            if h == 0:
+            if h == 0 and (nm, b) not in qkt:
                 qkt[(nm, b)] = trp.tile([P, 2048], BF16, name="%st%d" % (nm, b), tag=nm)
             words = qkt[(nm, b)][:].bitcast(F32).rearrange("p (u c) -> p u c", u=2)
             dst = words[:, :, 256 * h : 256 * h + 256]
@@ -117,6 +121,17 @@ def tile_scaleddotproductattention_t_kernel(tc, query_in, key_in, value_in, out)
                 nc.scalar.copy(out=dst, in_=src)
             else:
                 nc.vector.tensor_copy(out=dst, in_=src)
+
+        def first_q(ii):
+            t = ps_o.tile([P, 2, P], F32, name="tq%d" % ii, tag="o")
+            for u in range(2):
+                nc.tensor.transpose(
+                    out=t[:, u, :], in_=q_first[ii][:].bitcast(F32)[:, 128 * u : 128 * u + 128], identity=ident_f[:]
+                )
+            if ii == 0:
+                qkt[("q", 0)] = trp.tile([P, 2048], BF16, name="qt0", tag="q")
+            words = qkt[("q", 0)][:].bitcast(F32).rearrange("p (u c) -> p u c", u=2)
+            nc.scalar.copy(out=words[:, :, 128 * ii : 128 * ii + 128], in_=t[:])
 
         def mm(n, j):
             b, i = divmod(n, 4)
@@ -258,16 +273,21 @@ def tile_scaleddotproductattention_t_kernel(tc, query_in, key_in, value_in, out)
             mean[b] = vkeep.tile([P, 512], F32, name="mean%d" % b, tag="mean")
             nc.scalar.copy(out=mean[b][:], in_=m_ps[b][:])
 
-        for g4 in range(4):
-            for x in range(4):
-                pt(g4, x)
-            warm_pe()
-            tcopy(g4, g4 % 2)
+        for x in range(4):
+            pt(0, x)
+        tcopy(0, 0)
+        warm_pe()
+        for x in range(4):
+            pt(1, x)
+        tcopy(1, 1)
+        first_q(0)
+        first_q(1)
+        warm_pe()
         for k in range(4):
             vreg(0, k, 1)
 
-        pt_groups = {0: [4, 5], 1: [6, 7], 2: []}
-        tc_groups = {0: [], 1: [4, 5], 2: [6], 3: [7]}
+        pt_groups = {0: [3], 1: [4, 5], 2: [6, 7]}
+        tc_groups = {0: [3], 1: [], 2: [4, 5], 3: [6, 7]}
         for n in range(NT + 4):
             ets = [(0, n - 2, t) for t in range(2)] if 0 <= n - 2 < NT else []
             groups = pt_groups.get(n, [n + 5] if n + 5 < NT else [])
@@ -275,7 +295,7 @@ def tile_scaleddotproductattention_t_kernel(tc, query_in, key_in, value_in, out)
             if n < 2:
                 gaps = [[], [], [], pts]
             else:
-                gaps = [[], pts[0:2], pts[2:4], ets]
+                gaps = [[], pts[0:2], pts[2:4], pts[4:] + ets]
             bm, ph = divmod(n, 4)
             if 0 <= n - 1 < NT:
                 maxs(n - 1)

@@ -120,7 +120,8 @@ def tile_scaleddotproductattention_t_kernel(tc, query_in, key_in, value_in, out)
             if eng == 0:
                 nc.scalar.copy(out=dst, in_=src)
             else:
-                nc.vector.tensor_copy(out=dst, in_=src)
+                for u in range(2):
+                    nc.vector.tensor_copy(out=dst[:, u], in_=src[:, u])
 
         def first_q(ii):
             t = ps_o.tile([P, 2, P], F32, name="tq%d" % ii, tag="o")
@@ -276,18 +277,18 @@ def tile_scaleddotproductattention_t_kernel(tc, query_in, key_in, value_in, out)
         for x in range(4):
             pt(0, x)
         tcopy(0, 0)
-        warm_pe()
         for x in range(4):
             pt(1, x)
         tcopy(1, 1)
         first_q(0)
-        first_q(1)
         warm_pe()
+        first_q(1)
         for k in range(4):
             vreg(0, k, 1)
 
         pt_groups = {0: [3], 1: [4, 5], 2: [6, 7]}
         tc_groups = {0: [3], 1: [], 2: [4, 5], 3: [6, 7]}
+        v_done = 4
         for n in range(NT + 4):
             ets = [(0, n - 2, t) for t in range(2)] if 0 <= n - 2 < NT else []
             groups = pt_groups.get(n, [n + 5] if n + 5 < NT else [])
@@ -321,25 +322,32 @@ def tile_scaleddotproductattention_t_kernel(tc, query_in, key_in, value_in, out)
                 if n == NT:
                     wtail = ps_m.tile([P, 512], F32, name="wtail", tag="m")
                 warm_pe(wtail)
-            if 0 <= n - 3 < NT:
+            if 0 <= n - 3 < NT and n != NT + 1:
                 ecopy(n - 3)
                 eq(n - 3)
+            if n == NT:
+                fin(n - 4)
+                ecopy(n - 2)
+                eq(n - 2)
             if n == 1:
                 for k in range(4):
                     vq(0, k)
-                vreg(1, 0, 0)
-                vreg(1, 1, 0)
-            if 4 <= n + 1 < NT:
-                vq((n + 1) // 4, (n + 1) % 4)
-            if n >= 1 and n + 5 < NT:
-                vreg((n + 5) // 4, (n + 5) % 4, 0)
+            if n in (1, 2):
+                for c in range(2 * n + 2, 2 * n + 4):
+                    vreg(c // 4, c % 4, 0)
+            if n >= 3:
+                for c in range(v_done, min(v_done + (2 if ph == 3 and bm > 0 else 1), NT)):
+                    vq(c // 4, c % 4)
+                    if c + 4 < NT:
+                        vreg((c + 4) // 4, (c + 4) % 4, 0)
+                    v_done = c + 1
             for g4 in tc_groups.get(n, [n + 4] if n + 4 < NT else []):
-                tcopy(g4, 0)
+                tcopy(g4, g4 % 2 if 2 <= n < 4 else 0)
             if ph == 3 and n < NT:
                 meancopy(bm)
             if 0 <= n - 1 < NT:
                 expo(n - 1)
-            if 0 <= n - 4 < NT:
+            if 0 <= n - 4 < NT and n != NT:
                 fin(n - 4)
             if 0 <= n - 2 < NT:
                 recip(n - 2)

@@ -32,7 +32,7 @@ def tile_scaleddotproductattention_t_kernel(tc, query_in, key_in, value_in, out)
         small = ctx.enter_context(tc.tile_pool(name="small", bufs=6))
         vpool = ctx.enter_context(tc.tile_pool(name="vpool", bufs=4))
         vkeep = ctx.enter_context(tc.tile_pool(name="vkeep", bufs=3))
-        opool = ctx.enter_context(tc.tile_pool(name="opool", bufs=3))
+        opool = ctx.enter_context(tc.tile_pool(name="opool", bufs=8))
         ps_s = ctx.enter_context(tc.psum_pool(name="ps_s", bufs=2))
         ps_t = ctx.enter_context(tc.psum_pool(name="ps_t", bufs=2))
         ps_e = ctx.enter_context(tc.psum_pool(name="ps_e", bufs=1))
@@ -81,7 +81,9 @@ def tile_scaleddotproductattention_t_kernel(tc, query_in, key_in, value_in, out)
                 t = load_rows(src, b, 0, 4, nm)
                 qk_sb[(nm, b, 0)] = (t, 0)
                 qk_sb[(nm, b, 1)] = (t, 2)
-            v_sb[b] = load_rows(value_in, b, 0, 4, "v")
+                if nm == "k" and b > 1:
+                    v_sb[b - 1] = load_rows(value_in, b - 1, 0, 4, "v")
+        v_sb[B - 1] = load_rows(value_in, B - 1, 0, 4, "v")
 
         qkt, tp = {}, {}
         s_ps, sc, nb, rs, rc, e_sb, et_ps, eg, ec, es, o_ps = {}, {}, {}, {}, {}, {}, {}, {}, {}, {}, {}
@@ -335,7 +337,7 @@ def tile_scaleddotproductattention_t_kernel(tc, query_in, key_in, value_in, out)
             if n in (1, 2):
                 for c in range(2 * n + 2, 2 * n + 4):
                     vreg(c // 4, c % 4, 0)
-            if n >= 3:
+            if n >= 4:
                 for c in range(v_done, min(v_done + (2 if ph == 3 and bm > 0 else 1), NT)):
                     vq(c // 4, c % 4)
                     if c + 4 < NT:

@@ -279,12 +279,14 @@ def tile_scaleddotproductattention_t_kernel(tc, query_in, key_in, value_in, out)
         for x in range(4):
             pt(0, x)
         tcopy(0, 0)
+        warm_pe()
         for x in range(4):
             pt(1, x)
         tcopy(1, 1)
         first_q(0)
         warm_pe()
         first_q(1)
+        warm_pe()
         for k in range(4):
             vreg(0, k, 1)
 
@@ -338,7 +340,7 @@ def tile_scaleddotproductattention_t_kernel(tc, query_in, key_in, value_in, out)
                 for c in range(2 * n + 2, 2 * n + 4):
                     vreg(c // 4, c % 4, 0)
             if n >= 4:
-                for c in range(v_done, min(v_done + (2 if ph == 3 and bm > 0 else 1), NT)):
+                for c in range(v_done, min(v_done + (2 if ph == 3 and bm < 3 else 1), NT)):
                     vq(c // 4, c % 4)
                     if c + 4 < NT:
                         vreg((c + 4) // 4, (c + 4) % 4, 0)

@@ -161,10 +161,12 @@ def tile_scaleddotproductattention_t_kernel(tc, query_in, key_in, value_in, out)
 
         def expo(n):
             e_sb[n] = work.tile([P, 512], BF16, name="e%d" % n, tag="e")
-            rs[n] = small.tile([P, 1], F32, name="rs%d" % n, tag="rs")
+            pair, r = divmod(n, 2)
+            if r == 0:
+                rs[pair] = small.tile([P, 2], F32, name="rs%d" % pair, tag="rs")
             nc.scalar.activation(
                 out=e_sb[n][:], in_=sc[n][:], func=ACT.Exp, bias=nb[n][:], scale=-1.0,
-                accum_out=rs[n][:],
+                accum_out=rs[pair][:, r : r + 1],
             )
 
         def et(n, t):
@@ -193,9 +195,9 @@ def tile_scaleddotproductattention_t_kernel(tc, query_in, key_in, value_in, out)
                 in_=eg[n][:].rearrange("p q t -> p (q t)"),
             )
 
-        def recip(n):
-            rc[n] = small.tile([P, 1], F32, name="rc%d" % n, tag="rc")
-            nc.vector.reciprocal(out=rc[n][:], in_=rs[n][:])
+        def recip(pair):
+            rc[pair] = small.tile([P, 2], F32, name="rc%d" % pair, tag="rc")
+            nc.vector.reciprocal(out=rc[pair][:], in_=rs[pair][:])
 
         def mx(n):
             b = n // 4
@@ -211,19 +213,23 @@ def tile_scaleddotproductattention_t_kernel(tc, query_in, key_in, value_in, out)
             b, i = divmod(n, 4)
             if i == 0:
                 osb[b] = opool.tile([P, 4, 512], F32, name="osb%d" % b, tag="osb")
-            nc.vector.scalar_tensor_tensor(
-                out=osb[b][:, i, :], in0=o_ps[n][:], scalar=rc[n][:], in1=mean[b][:],
-                op0=ALU.mult, op1=ALU.subtract,
-            )
+            view = out[b].rearrange("(p i) d -> p i d", i=4)
+            pair, r = divmod(n, 2)
+            halves = [slice(0, 256), slice(256, 512)] if n == NT - 1 else [slice(0, 512)]
+            for cols in halves:
+                nc.vector.scalar_tensor_tensor(
+                    out=osb[b][:, i, cols], in0=o_ps[n][:, cols], scalar=rc[pair][:, r : r + 1],
+                    in1=mean[b][:, cols], op0=ALU.mult, op1=ALU.subtract,
+                )
+                if n == NT - 1:
+                    nc.sync.dma_start(out=view[:, i, cols], in_=osb[b][:, i, cols])
             if b < B - 1:
                 spans = {3: (0, 4)}
             else:
-                spans = {1: (0, 2), 2: (2, 3), 3: (3, 4)}
+                spans = {1: (0, 2), 2: (2, 3)}
             if i in spans:
                 i0, i1 = spans[i]
-                nc.sync.dma_start(
-                    out=out[b].rearrange("(p i) d -> p i d", i=4)[:, i0:i1, :], in_=osb[b][:, i0:i1, :]
-                )
+                nc.sync.dma_start(out=view[:, i0:i1, :], in_=osb[b][:, i0:i1, :])
 
         def vreg(b, k, eng):
             vg[(b, k)] = vpool.tile([P, 128, 4], BF16, name="vg%d_%d" % (b, k), tag="vg", align_bytes=64)
@@ -353,5 +359,5 @@ def tile_scaleddotproductattention_t_kernel(tc, query_in, key_in, value_in, out)
                 expo(n - 1)
             if 0 <= n - 4 < NT and n != NT:
                 fin(n - 4)
-            if 0 <= n - 2 < NT:
-                recip(n - 2)
+            if 0 <= n - 2 < NT and n % 2 == 1:
+                recip((n - 2) // 2)

@@ -322,12 +322,12 @@ def tile_scaleddotproductattention_t_kernel(tc, query_in, key_in, value_in, out)
                         et(a, x)
                     else:
                         pt(a, x)
+                if ph < 2 and n < NT and (j in (1, 2) if n >= 4 else j == 3):
+                    for c in ([2 * ph + j - 1] if n >= 4 else [2 * ph, 2 * ph + 1]):
+                        msum(bm, c)
                 if j == 3 and ph == 2 and n < NT:
                     for c in range(4):
                         mbc(bm, c)
-            if ph < 2 and n < NT:
-                msum(bm, 2 * ph)
-                msum(bm, 2 * ph + 1)
             if NT <= n < NT + 3:
                 if n == NT:
                     wtail = ps_m.tile([P, 512], F32, name="wtail", tag="m")

from contextlib import ExitStack
import math

import concourse.mybir as mybir
from concourse.masks import make_identity

B, T, D = 8, 512, 512
FLOPS = 2 * 2 * B * T * T * D

P = 128
NT = 4 * B
BF16 = mybir.dt.bfloat16
F32 = mybir.dt.float32
U32 = mybir.dt.uint32
U8 = mybir.dt.uint8
FP8X4 = mybir.dt.float8_e4m3fn_x4
ALU = mybir.AluOpType
ACT = mybir.ActivationFunctionType
AX = mybir.AxisListType
GP = 4
NG = P // GP
SCALE = 1.0 / math.sqrt(D)


def tile_scaleddotproductattention_t_kernel(tc, query_in, key_in, value_in, out):
    nc = tc.nc
    with ExitStack() as ctx:
        const = ctx.enter_context(tc.tile_pool(name="const", bufs=1))
        inp = ctx.enter_context(tc.tile_pool(name="inp", bufs=1))
        trp = ctx.enter_context(tc.tile_pool(name="trp", bufs=2))
        work = ctx.enter_context(tc.tile_pool(name="work", bufs=3))
        small = ctx.enter_context(tc.tile_pool(name="small", bufs=6))
        vpool = ctx.enter_context(tc.tile_pool(name="vpool", bufs=4))
        vkeep = ctx.enter_context(tc.tile_pool(name="vkeep", bufs=3))
        opool = ctx.enter_context(tc.tile_pool(name="opool", bufs=8))
        ps_s = ctx.enter_context(tc.psum_pool(name="ps_s", bufs=2))
        ps_t = ctx.enter_context(tc.psum_pool(name="ps_t", bufs=2))
        ps_e = ctx.enter_context(tc.psum_pool(name="ps_e", bufs=1))
        ps_o = ctx.enter_context(tc.psum_pool(name="ps_o", bufs=2))
        ps_m = ctx.enter_context(tc.psum_pool(name="ps_m", bufs=1))
        ctx.enter_context(tc.manual_schedule())

        wz = const.tile([P, P], F32, name="wz")
        nc.vector.memset(wz[:], 0.0)
        wps = ps_e.tile([P, P], F32, name="wps", tag="et")

        def warm_pe(ps=wps):
            nc.tensor.matmul(out=ps[:, 0:P], lhsT=wz[:], rhs=wz[:], start=True, stop=True)

        for w in range(4):
            warm_pe()

        ident_f = const.tile([P, P], F32, name="ident_f")
        make_identity(nc, ident_f[:])
        sel_f = const.tile([P, NG], F32, name="sel_f")
        nc.vector.tensor_reduce(
            out=sel_f[:], in_=ident_f[:].rearrange("p (g j) -> p g j", j=GP), axis=AX.X, op=ALU.add
        )
        sel = const.tile([P, NG], BF16, name="sel")
        nc.vector.tensor_scalar(out=sel[:], in0=sel_f[:], scalar1=1.0 / T, scalar2=None, op0=ALU.mult)
        warm = const.tile([P, 1], F32, name="warm")
        nc.vector.memset(warm[:], 0.0)
        warm2 = const.tile([P, 1], F32, name="warm2")
        nc.scalar.activation(out=warm2[:], in_=warm[:], func=ACT.Exp)

        qk_sb, v_sb = {}, {}

        def load_rows(src, b, i0, i1, nm):
            t = inp.tile([P, (i1 - i0) * D], BF16, name="%s%d_%d" % (nm, b, i0))
            view = src[b].rearrange("(p i) d -> p (i d)", i=4)
            nc.sync.dma_start(out=t[:], in_=view[:, i0 * D : i1 * D])
            return t

        for h in range(2):
            qk_sb[("k", 0, h)] = (load_rows(key_in, 0, 2 * h, 2 * h + 2, "k"), 0)
        q_first = [load_rows(query_in, 0, ii, ii + 1, "q") for ii in range(2)]
        qk_sb[("q", 0, 1)] = (load_rows(query_in, 0, 2, 4, "q"), 0)
        v_sb[0] = load_rows(value_in, 0, 0, 4, "v")
        for b in range(1, B):
            for nm, src in (("k", key_in), ("q", query_in)):
                t = load_rows(src, b, 0, 4, nm)
                qk_sb[(nm, b, 0)] = (t, 0)
                qk_sb[(nm, b, 1)] = (t, 2)
                if nm == "k" and b > 1:
                    v_sb[b - 1] = load_rows(value_in, b - 1, 0, 4, "v")
        v_sb[B - 1] = load_rows(value_in, B - 1, 0, 4, "v")

        qkt, tp = {}, {}
        s_ps, sc, nb, rs, rc, e_sb, et_ps, eg, ec, es, o_ps = {}, {}, {}, {}, {}, {}, {}, {}, {}, {}, {}
        vg, vc, vs, mcol, m_ps, mean, osb = {}, {}, {}, {}, {}, {}, {}

        def group(g4):
            b, g = divmod(g4, 4)
            return ("k" if g < 2 else "q"), b, g % 2

        def pt(g4, x):
            nm, b, h = group(g4)
            u, ii = divmod(x, 2)
            src, i0 = qk_sb[(nm, b, h)]
            col = 256 * (i0 + ii) + 128 * u
            if x == 0:
                if g4 in (6, 7):
                    tp[g4] = ps_o.tile([P, 512], F32, name="tp%d" % g4, tag="o")
                else:
                    tp[g4] = ps_t.tile([P, 512], F32, name="tp%d" % g4, tag="tp")
            nc.tensor.transpose(
                out=tp[g4][:, 128 * x : 128 * x + 128],
                in_=src[:].bitcast(F32)[:, col : col + 128],
                identity=ident_f[:],
            )

        def tcopy(g4, eng):
            nm, b, h = group(g4)
            if h == 0 and (nm, b) not in qkt:
                qkt[(nm, b)] = trp.tile([P, 2048], BF16, name="%st%d" % (nm, b), tag=nm)
            words = qkt[(nm, b)][:].bitcast(F32).rearrange("p (u c) -> p u c", u=2)
            dst = words[:, :, 256 * h : 256 * h + 256]
            src = tp[g4][:].rearrange("p (u c) -> p u c", u=2)
            if nm == "k":
                dst = dst.rearrange("p u (c i) -> p u c i", i=2)
                src = tp[g4][:].rearrange("p (u i c) -> p u c i", u=2, i=2)
            if eng == 0:
                nc.scalar.copy(out=dst, in_=src)
            else:
                for u in range(2):
                    nc.vector.tensor_copy(out=dst[:, u], in_=src[:, u])

        def first_q(ii):
            t = ps_o.tile([P, 2, P], F32, name="tq%d" % ii, tag="o")
            for u in range(2):
                nc.tensor.transpose(
                    out=t[:, u, :], in_=q_first[ii][:].bitcast(F32)[:, 128 * u : 128 * u + 128], identity=ident_f[:]
                )
            if ii == 0:
                qkt[("q", 0)] = trp.tile([P, 2048], BF16, name="qt0", tag="q")
            words = qkt[("q", 0)][:].bitcast(F32).rearrange("p (u c) -> p u c", u=2)
            nc.scalar.copy(out=words[:, :, 128 * ii : 128 * ii + 128], in_=t[:])

        def mm(n, j):
            b, i = divmod(n, 4)
            u, e = divmod(j, 2)
            if j == 0:
                s_ps[n] = ps_s.tile([P, 512], F32, name="s%d" % n, tag="s")
            qv = qkt[("q", b)][:].rearrange("p (u c e) -> p u c e", u=2, e=2)
            kv = qkt[("k", b)][:].rearrange("p (u c e) -> p u c e", u=2, e=2)
            nc.tensor.matmul(
                out=s_ps[n][:],
                lhsT=qv[:, u, 128 * i : 128 * i + 128, e],
                rhs=kv[:, u, :, e],
                start=(j == 0),
                stop=(j == 3),
            )

        def maxs(n):
            sc[n] = work.tile([P, 512], F32, name="sc%d" % n, tag="sc")
            nb[n] = small.tile([P, 1], F32, name="nb%d" % n, tag="nb")
            nc.vector.tensor_scalar(
                out=sc[n][:], in0=s_ps[n][:], scalar1=-SCALE, scalar2=None,
                op0=ALU.mult, op1=ALU.min, accum_out=nb[n][:],
            )

        def expo(n):
            e_sb[n] = work.tile([P, 512], BF16, name="e%d" % n, tag="e")
            pair, r = divmod(n, 2)
            if r == 0:
                rs[pair] = small.tile([P, 2], F32, name="rs%d" % pair, tag="rs")
            nc.scalar.activation(
                out=e_sb[n][:], in_=sc[n][:], func=ACT.Exp, bias=nb[n][:], scale=-1.0,
                accum_out=rs[pair][:, r : r + 1],
            )

        def et(n, t):
            if t == 0:
                if n >= NT - 5 and n % 2 == 1:
                    et_ps[n] = ps_t.tile([P, 2, P], F32, name="et%d" % n, tag="tp")
                else:
                    et_ps[n] = ps_e.tile([P, 2, P], F32, name="et%d" % n, tag="et")
            nc.tensor.transpose(
                out=et_ps[n][:, t, :], in_=e_sb[n][:].bitcast(F32)[:, 128 * t : 128 * t + 128],
                identity=ident_f[:],
            )

        def ecopy(n):
            eg[n] = work.tile([P, P, 4], BF16, name="eg%d" % n, tag="eg", align_bytes=64)
            nc.scalar.copy(
                out=eg[n][:].rearrange("p q t -> p (q t)").bitcast(F32).rearrange("p (q h) -> p q h", h=2),
                in_=et_ps[n][:].rearrange("p h q -> p q h"),
            )

        def eq(n):
            ec[n] = work.tile([P, P], U32, name="ec%d" % n, tag="ec", align_bytes=64)
            es[n] = work.tile([P, P], U8, name="es%d" % n, tag="es", align_bytes=64)
            nc.vector.quantize_mx(
                out=ec[n][:].bitcast(FP8X4), scales=es[n][:],
                in_=eg[n][:].rearrange("p q t -> p (q t)"),
            )

        def recip(pair):
            rc[pair] = small.tile([P, 2], F32, name="rc%d" % pair, tag="rc")
            nc.vector.reciprocal(out=rc[pair][:], in_=rs[pair][:])

        def mx(n):
            b = n // 4
            o_ps[n] = ps_o.tile([P, 512], F32, name="o%d" % n, tag="o")
            nc.tensor.matmul_mx(
                out=o_ps[n][:],
                lhsT=ec[n][:].bitcast(FP8X4), lhsT_scale=es[n][:],
                rhs=vc[b][:].bitcast(FP8X4), rhs_scale=vs[b][:],
                start=True, stop=True,
            )

        def fin(n):
            b, i = divmod(n, 4)
            if i == 0:
                osb[b] = opool.tile([P, 4, 512], F32, name="osb%d" % b, tag="osb")
            view = out[b].rearrange("(p i) d -> p i d", i=4)
            pair, r = divmod(n, 2)
            halves = [slice(0, 256), slice(256, 512)] if n == NT - 1 else [slice(0, 512)]
            for cols in halves:
                nc.vector.scalar_tensor_tensor(
                    out=osb[b][:, i, cols], in0=o_ps[n][:, cols], scalar=rc[pair][:, r : r + 1],
                    in1=mean[b][:, cols], op0=ALU.mult, op1=ALU.subtract,
                )
                if n == NT - 1:
                    nc.sync.dma_start(out=view[:, i, cols], in_=osb[b][:, i, cols])
            if b < B - 1:
                spans = {3: (0, 4)}
            else:
                spans = {1: (0, 2), 2: (2, 3)}
            if i in spans:
                i0, i1 = spans[i]
                nc.sync.dma_start(out=view[:, i0:i1, :], in_=osb[b][:, i0:i1, :])

        def vreg(b, k, eng):
            vg[(b, k)] = vpool.tile([P, 128, 4], BF16, name="vg%d_%d" % (b, k), tag="vg", align_bytes=64)
            src = v_sb[b][:].rearrange("p (t d) -> p t d", t=4)[:, :, 128 * k : 128 * k + 128]
            if eng == 1:
                nc.vector.tensor_copy(
                    out=vg[(b, k)][:].rearrange("p (c i) t -> p c t i", i=4),
                    in_=src.rearrange("p t (c i) -> p c t i", i=4),
                )
            else:
                nc.gpsimd.tensor_scalar(
                    out=vg[(b, k)][:], in0=src.rearrange("p t d -> p d t"), scalar1=1.0, scalar2=0.0,
                    op0=ALU.mult, op1=ALU.add,
                )

        def vq(b, k):
            if k == 0:
                vc[b] = vkeep.tile([P, 512], U32, name="vc%d" % b, tag="vc", align_bytes=64)
                vs[b] = vkeep.tile([P, 512], U8, name="vs%d" % b, tag="vs", align_bytes=64)
            cols = slice(128 * k, 128 * k + 128)
            nc.vector.quantize_mx(
                out=vc[b][:, cols].bitcast(FP8X4), scales=vs[b][:, cols],
                in_=vg[(b, k)][:].rearrange("p d t -> p (d t)"),
            )

        def msum(b, c):
            if c == 0:
                m_ps[b] = ps_m.tile([P, 512], F32, name="m%d" % b, tag="m")
            for t in range(4):
                col = 512 * t + 128 * c
                nc.tensor.matmul(
                    out=m_ps[b][:, NG * c : NG * c + NG], lhsT=v_sb[b][:, col : col + 128], rhs=sel[:],
                    start=(t == 0), stop=(t == 3),
                )

        def mred(b):
            mcol[b] = small.tile([P, 4], F32, name="mcol%d" % b, tag="mcol")
            nc.vector.tensor_reduce(
                out=mcol[b][:], in_=m_ps[b][:, 0 : 4 * NG].rearrange("p (c g) -> p c g", g=NG),
                axis=AX.X, op=ALU.add,
            )

        def mbc(b, c):
            nc.tensor.transpose(
                out=m_ps[b][:, 128 * c : 128 * c + 128], in_=mcol[b][:, c : c + 1].to_broadcast([P, P]),
                identity=ident_f[:],
            )

        def meancopy(b):
            mean[b] = vkeep.tile([P, 512], F32, name="mean%d" % b, tag="mean")
            nc.scalar.copy(out=mean[b][:], in_=m_ps[b][:])

        for x in range(4):
            pt(0, x)
        tcopy(0, 0)
        warm_pe()
        for x in range(4):
            pt(1, x)
        tcopy(1, 1)
        first_q(0)
        warm_pe()
        first_q(1)
        warm_pe()
        for k in range(4):
            vreg(0, k, 1)

        pt_groups = {0: [3], 1: [4, 5], 2: [6, 7]}
        tc_groups = {0: [3], 1: [], 2: [4, 5], 3: [6, 7]}
        v_done = 4
        for n in range(NT + 4):
            ets = [(0, n - 2, t) for t in range(2)] if 0 <= n - 2 < NT else []
            groups = pt_groups.get(n, [n + 5] if n + 5 < NT else [])
            pts = [(1, g4, x) for g4 in groups for x in range(4)]
            if n < 2:
                gaps = [[], [], [], pts]
            else:
                gaps = [[], pts[0:2], pts[2:4], pts[4:] + ets]
            bm, ph = divmod(n, 4)
            if 0 <= n - 1 < NT:
                maxs(n - 1)
            if ph == 2 and n < NT:
                mred(bm)
            for j in range(4):
                if n < NT:
                    mm(n, j)
                if j == 0 and 0 <= n - 4 < NT:
                    mx(n - 4)
                for kind, a, x in gaps[j]:
                    if kind == 0:
                        et(a, x)
                    else:
                        pt(a, x)
                if ph < 2 and n < NT and (j in (1, 2) if n >= 4 else j == 3):
                    for c in ([2 * ph + j - 1] if n >= 4 else [2 * ph, 2 * ph + 1]):
                        msum(bm, c)
                if j == 3 and ph == 2 and n < NT:
                    for c in range(4):
                        mbc(bm, c)
            if NT <= n < NT + 3:
                if n == NT:
                    wtail = ps_m.tile([P, 512], F32, name="wtail", tag="m")
                warm_pe(wtail)
            if 0 <= n - 3 < NT and n != NT + 1:
                ecopy(n - 3)
                eq(n - 3)
            if n == NT:
                fin(n - 4)
                ecopy(n - 2)
                eq(n - 2)
            if n == 1:
                for k in range(4):
                    vq(0, k)
            if n in (1, 2):
                for c in range(2 * n + 2, 2 * n + 4):
                    vreg(c // 4, c % 4, 0)
            if n >= 4:
                for c in range(v_done, min(v_done + (2 if ph == 3 and bm < 3 else 1), NT)):
                    vq(c // 4, c % 4)
                    if c + 4 < NT:
                        vreg((c + 4) // 4, (c + 4) % 4, 0)
                    v_done = c + 1
            for g4 in tc_groups.get(n, [n + 4] if n + 4 < NT else []):
                tcopy(g4, g4 % 2 if 2 <= n < 4 else 0)
            if ph == 3 and n < NT:
                meancopy(bm)
            if 0 <= n - 1 < NT:
                expo(n - 1)
            if 0 <= n - 4 < NT and n != NT:
                fin(n - 4)
            if 0 <= n - 2 < NT and n % 2 == 1:
                recip((n - 2) // 2)
